import numpy as np
import ml_dtypes


def mxq(x, axis, fmt="e4m3"):
    dtype, down = {"e4m3": (ml_dtypes.float8_e4m3fn, 7), "e5m2": (ml_dtypes.float8_e5m2, 14)}[fmt]
    v = np.moveaxis(np.asarray(x, np.float32).astype(ml_dtypes.bfloat16).astype(np.float64), axis, -1)
    blocks = v.reshape(v.shape[:-1] + (-1, 32))
    amax = np.abs(blocks).max(-1, keepdims=True)
    byte = np.maximum(np.where(amax > 0, np.frexp(amax)[1] - 1 + 127, 0) - down, 1)
    scale = np.exp2(byte - 127.0)
    codes = (blocks / scale).astype(np.float32).astype(dtype).astype(np.float64)
    return np.moveaxis((codes * scale).reshape(v.shape), -1, axis)


WIDE = False


def mx_kscale(k):
    if not WIDE:
        return np.ones(k)
    levels = np.array([10, -10, 5, -5, 0])
    a = np.random.permutation(np.resize(levels, k // 512 * 4)).reshape(k // 512, 4)
    idx = np.arange(k)
    return np.exp2(a[idx // 512, idx % 128 // 32])


BF16 = ml_dtypes.bfloat16


def bf(x):
    return np.asarray(x, np.float32).astype(BF16)


def f64(x):
    return np.asarray(x).astype(np.float64)


N, D = 512, 4096
BLOCK, GROUP = 32, 512


def draw(s, two_levels):
    u = np.random.uniform(1e-3, 1.0, (N, D))
    if s.max() == s.min():
        return bf(u * 4.0 / np.sqrt(D))
    p = (0.5 + 0.5 * u) * 2.0**-18
    if two_levels:
        p = p * np.where(np.random.rand(N, D) < 0.5, 1.0, 2.0**-90)
    one = np.zeros((D // GROUP, GROUP // BLOCK), bool)
    one[np.arange(D // GROUP), s.reshape(D // GROUP, GROUP).argmax(1) // BLOCK] = True
    one = np.repeat(one.reshape(-1), BLOCK)
    one[::BLOCK] = False
    p[:, one] = 1.0
    return bf(p)


def setup_inputs():
    s = mx_kscale(D)
    return {"new_source": draw(s, True), "new_target": draw(s, False)}


def _pairwise_kl(p):
    logp = np.log(p)
    self_term = np.sum(p * logp, axis=-1)
    cross = mxq(p, 1, "e4m3") @ mxq(logp, 1, "e4m3").T
    return self_term[:, None] - cross


def reference(new_source, new_target):
    n = new_source.shape[0]
    a = _pairwise_kl(f64(new_source))
    b = _pairwise_kl(f64(new_target))
    return (1e-4 + np.sum(np.abs(a - b))) / (n * n)

@@ -1,0 +1,215 @@
+from contextlib import ExitStack
+
+import concourse.mybir as mybir
+from concourse.masks import make_identity
+
+F32 = mybir.dt.float32
+BF16 = mybir.dt.bfloat16
+U32 = mybir.dt.uint32
+U8 = mybir.dt.uint8
+FP8X4 = mybir.dt.float8_e4m3fn_x4
+ACT = mybir.ActivationFunctionType
+ALU = mybir.AluOpType
+AX = mybir.AxisListType
+
+P = 128
+N_ROWS = 512
+D = 4096
+RT = N_ROWS // P
+KP = 512
+G = D // KP
+UNITS = 2 * G
+FLOPS = 2 * 2 * N_ROWS * N_ROWS * D
+
+LN_SCALE = 2.0**62
+
+
+def tile_self_l1_kernel(tc, new_source, new_target, out):
+    nc = tc.nc
+    with ExitStack() as ctx:
+        const = ctx.enter_context(tc.tile_pool(name="const", bufs=1))
+        xpool = ctx.enter_context(tc.tile_pool(name="xpool", bufs=1))
+        lpool = ctx.enter_context(tc.tile_pool(name="lpool", bufs=3))
+        gpool = ctx.enter_context(tc.tile_pool(name="gpool", bufs=3))
+        qpool = ctx.enter_context(tc.tile_pool(name="qpool", bufs=3))
+        tpool = ctx.enter_context(tc.psum_pool(name="tpool", bufs=4))
+        apool = ctx.enter_context(tc.psum_pool(name="apool", bufs=1))
+        ctx.enter_context(tc.manual_schedule())
+
+        x_src = xpool.tile([P, G, RT, KP], BF16)
+        x_tgt = xpool.tile([P, G, RT, KP], BF16)
+        x = (x_src, x_tgt)
+        for mat, dram in enumerate((new_source, new_target)):
+            view = dram.rearrange("(rt p) (g w) -> p g rt w", p=P, w=KP)
+            for g in range(G):
+                nc.sync.dma_start(out=x[mat][:, g], in_=view[:, g])
+
+        unit = const.tile([P, 1], F32)
+        nc.vector.memset(unit[:], 1.0)
+        shift = const.tile([P, 1], F32)
+        nc.scalar.activation(out=shift[:], in_=unit[:], func=ACT.Ln, scale=LN_SCALE)
+        ident = const.tile([P, P], F32)
+        make_identity(nc, ident[:])
+        ones = const.tile([P, P], F32)
+        nc.vector.memset(ones[:], 1.0)
+        sp = const.tile([P, 2, RT, 8], F32)
+        nc.vector.memset(sp[:], 0.0)
+        selfs = const.tile([P, 2, RT], F32)
+        ds = const.tile([P, RT], F32)
+        cs = const.tile([P, RT, N_ROWS], F32)
+        xd = const.tile([P, RT, N_ROWS], F32)
+        parts = const.tile([P, RT], F32)
+        tot1 = const.tile([P, 1], F32)
+        res = const.tile([P, 1], F32)
+
+        items = []
+        for g in range(4):
+            items.append(("unit", 0, g, 0, g))
+        for rt in range(RT):
+            items.append(("row", 0, rt, 4, 4))
+        for half in range(2):
+            for rt in range(RT):
+                items.append(("row", 1, rt, 4 * half, half))
+        logs = {}
+
+        def nat_act(j):
+            kind, mat, a, g0, slot = items[j]
+            l32 = lpool.tile([P, 4, KP], F32)
+            if kind == "unit":
+                src = x[mat][:, a]
+            else:
+                src = x[mat][:, g0 : g0 + 4, a, :]
+            nc.scalar.activation(out=l32[:], in_=src, func=ACT.Ln, scale=LN_SCALE)
+            logs[j] = l32
+
+        def nat_dve(j):
+            kind, mat, a, g0, slot = items[j]
+            l32 = logs[j]
+            if kind == "unit":
+                for rt in range(RT):
+                    nc.vector.scalar_tensor_tensor(
+                        out=l32[:, rt, :], in0=l32[:, rt, :], scalar=shift[:, 0:1], in1=x[mat][:, a, rt, :],
+                        op0=ALU.subtract, op1=ALU.mult, accum_out=sp[:, mat, rt, slot : slot + 1],
+                    )
+            else:
+                nc.vector.scalar_tensor_tensor(
+                    out=l32[:], in0=l32[:], scalar=shift[:, 0:1], in1=x[mat][:, g0 : g0 + 4, a, :],
+                    op0=ALU.subtract, op1=ALU.mult, accum_out=sp[:, mat, a, slot : slot + 1],
+                )
+
+        banks = {}
+        gps = {}
+        gls = {}
+        lts = {}
+        pq = {}
+        lq = {}
+        acc = {}
+
+        def transposes(u):
+            mat, g = divmod(u, G)
+            pair = []
+            for h in range(2):
+                tp = tpool.tile([P, 2, 2 * P], F32)
+                for j in range(2):
+                    words = x[mat][:, g, 2 * h + j, :].bitcast(F32).rearrange("p (w u) -> p w u", u=2)
+                    for uu in range(2):
+                        nc.tensor.transpose(tp[:, uu, P * j : P * j + P], words[:, :, uu], ident[:])
+                pair.append(tp)
+            banks[u] = pair
+
+        def copy_out(u):
+            gp = gpool.tile([P, 4 * N_ROWS], BF16, align_bytes=64)
+            gw = gp[:].bitcast(F32).rearrange("p (r u) -> p r u", u=2)
+            for h in range(2):
+                dst = gw[:, 256 * h : 256 * h + 256, :]
+                src = banks[u][h][:].rearrange("p u r -> p r u")
+                if u >= 2 and (h == 1 or u % 4 == 0):
+                    nc.scalar.copy(out=dst, in_=src)
+                else:
+                    nc.vector.tensor_copy(out=dst, in_=src)
+            gps[u] = gp
+
+        def log_t(u):
+            lt = lpool.tile([P, 4 * N_ROWS], F32)
+            nc.scalar.activation(out=lt[:], in_=gps[u][:], func=ACT.Ln, scale=LN_SCALE)
+            lts[u] = lt
+
+        def fix(u):
+            gl = gpool.tile([P, 4 * N_ROWS], BF16, align_bytes=64)
+            nc.vector.tensor_scalar(
+                out=gl[:], in0=lts[u][:], scalar1=shift[:, 0:1], scalar2=None, op0=ALU.subtract
+            )
+            gls[u] = gl
+
+        def quant(src, store, u):
+            codes = qpool.tile([P, N_ROWS], U32, align_bytes=64, tag="codes" + store[0], name="codes")
+            scales = qpool.tile([P, N_ROWS], U8, align_bytes=64, tag="scales" + store[0], name="scales")
+            nc.vector.quantize_mx(out=codes[:].bitcast(FP8X4), scales=scales[:], in_=src[:])
+            store[1][u] = (codes, scales)
+
+        def passes(u):
+            mat, g = divmod(u, G)
+            if g == 0:
+                for m in range(RT):
+                    acc[m] = apool.tile([P, N_ROWS], F32, tag="acc%d" % m, name="acc%d" % m)
+            pc, ps = pq[u]
+            lc, ls = lq[u]
+            for m in range(RT):
+                cols = slice(P * m, P * m + P)
+                nc.tensor.matmul_mx(
+                    out=acc[m][:],
+                    lhsT=pc[:, cols].bitcast(FP8X4), lhsT_scale=ps[:, cols],
+                    rhs=lc[:].bitcast(FP8X4), rhs_scale=ls[:],
+                    start=(g == 0), stop=(g == G - 1),
+                )
+
+        transposes(0)
+        transposes(1)
+        nat_act(0)
+        nat_act(1)
+        copy_out(0)
+        nat_dve(0)
+        quant(gps[0], ("p", pq), 0)
+        for u in range(UNITS):
+            if u + 2 < UNITS:
+                transposes(u + 2)
+            if u + 1 < UNITS:
+                copy_out(u + 1)
+            log_t(u)
+            if u == G:
+                for m in range(RT):
+                    if m < 2:
+                        nc.vector.tensor_copy(out=cs[:, m, :], in_=acc[m][:])
+                    else:
+                        nc.scalar.copy(out=cs[:, m, :], in_=acc[m][:])
+            if u + 1 < len(items):
+                nat_dve(u + 1)
+            if u + 2 < len(items):
+                nat_act(u + 2)
+            fix(u)
+            if u + 1 < UNITS:
+                quant(gps[u + 1], ("p", pq), u + 1)
+            quant(gls[u], ("l", lq), u)
+            passes(u)
+
+        nc.vector.tensor_reduce(out=selfs[:], in_=sp[:], axis=AX.X, op=ALU.add)
+        nc.vector.tensor_sub(out=ds[:], in0=selfs[:, 0, :], in1=selfs[:, 1, :])
+        for m in range(RT):
+            nc.vector.scalar_tensor_tensor(
+                out=xd[:, m, :], in0=acc[m][:], scalar=ds[:, m : m + 1], in1=cs[:, m, :],
+                op0=ALU.add, op1=ALU.subtract,
+            )
+            nc.scalar.activation(
+                out=xd[:, m, :], in_=xd[:, m, :], func=ACT.Abs, accum_out=parts[:, m : m + 1]
+            )
+        tot = tpool.tile([P, 2, 2 * P], F32, tag="tp", name="tot")
+        nc.tensor.matmul(out=tot[:, 0, 0:RT], lhsT=ones[:], rhs=parts[:], start=True, stop=True)
+        nc.vector.tensor_reduce(out=tot1[:], in_=tot[:, 0, 0:RT], axis=AX.X, op=ALU.add)
+        nc.vector.tensor_scalar(
+            out=res[:], in0=tot1[:], scalar1=1e-4, scalar2=1.0 / (N_ROWS * N_ROWS),
+            op0=ALU.add, op1=ALU.mult,
+        )
+        dst = out
+        while dst.ndim < 2:
+            dst = dst.unsqueeze(0)
+        nc.sync.dma_start(out=dst, in_=res[0:1, 0:1])

@@ -22,6 +22,7 @@ UNITS = 2 * G
 FLOPS = 2 * 2 * N_ROWS * N_ROWS * D
 
 LN_SCALE = 2.0**62
+ACT_FIRST_BANK = (3, 6, 9, 12, 15)
 
 
 def tile_self_l1_kernel(tc, new_source, new_target, out):
@@ -29,6 +30,7 @@ def tile_self_l1_kernel(tc, new_source, new_target, out):
     with ExitStack() as ctx:
         const = ctx.enter_context(tc.tile_pool(name="const", bufs=1))
         xpool = ctx.enter_context(tc.tile_pool(name="xpool", bufs=1))
+        npool = ctx.enter_context(tc.tile_pool(name="npool", bufs=4))
         lpool = ctx.enter_context(tc.tile_pool(name="lpool", bufs=3))
         gpool = ctx.enter_context(tc.tile_pool(name="gpool", bufs=3))
         qpool = ctx.enter_context(tc.tile_pool(name="qpool", bufs=3))
@@ -42,7 +44,11 @@ def tile_self_l1_kernel(tc, new_source, new_target, out):
         for mat, dram in enumerate((new_source, new_target)):
             view = dram.rearrange("(rt p) (g w) -> p g rt w", p=P, w=KP)
             for g in range(G):
-                nc.sync.dma_start(out=x[mat][:, g], in_=view[:, g])
+                if mat == 0 and g == 0:
+                    nc.sync.dma_start(out=x[0][:, 0, 0:2], in_=view[:, 0, 0:2])
+                    nc.sync.dma_start(out=x[0][:, 0, 2:4], in_=view[:, 0, 2:4])
+                else:
+                    nc.sync.dma_start(out=x[mat][:, g], in_=view[:, g])
 
         unit = const.tile([P, 1], F32)
         nc.vector.memset(unit[:], 1.0)
@@ -50,51 +56,56 @@ def tile_self_l1_kernel(tc, new_source, new_target, out):
         nc.scalar.activation(out=shift[:], in_=unit[:], func=ACT.Ln, scale=LN_SCALE)
         ident = const.tile([P, P], F32)
         make_identity(nc, ident[:])
-        ones = const.tile([P, P], F32)
-        nc.vector.memset(ones[:], 1.0)
+        mean_w = const.tile([P, P], F32)
+        nc.vector.memset(mean_w[:], 1.0 / (N_ROWS * N_ROWS))
         sp = const.tile([P, 2, RT, 8], F32)
         nc.vector.memset(sp[:], 0.0)
+        parts = const.tile([P, 16], F32)
+        nc.vector.memset(parts[:], 0.0)
+        nc.vector.memset(parts[:, 15:16], 1e-4 / P)
         selfs = const.tile([P, 2, RT], F32)
         ds = const.tile([P, RT], F32)
-        cs = const.tile([P, RT, N_ROWS], F32)
-        xd = const.tile([P, RT, N_ROWS], F32)
-        parts = const.tile([P, RT], F32)
-        tot1 = const.tile([P, 1], F32)
+        junk_a = const.tile([P, N_ROWS], F32)
+        xd = const.tile([P, N_ROWS], F32)
+        junk_v = const.tile([P, N_ROWS], F32)
         res = const.tile([P, 1], F32)
 
-        items = []
-        for g in range(4):
-            items.append(("unit", 0, g, 0, g))
-        for rt in range(RT):
-            items.append(("row", 0, rt, 4, 4))
-        for half in range(2):
+        items = [(0, 0, 2, 0, 1, 0), (0, 2, 2, 0, 1, 0), (0, 0, 4, 1, 1, 1)]
+        for g0, slot in ((2, 2), (5, 3)):
             for rt in range(RT):
-                items.append(("row", 1, rt, 4 * half, half))
+                items.append((0, rt, 1, g0, 3, slot))
+        for g0, slot in ((0, 0), (4, 1)):
+            for rt in range(RT):
+                items.append((1, rt, 1, g0, 4, slot))
         logs = {}
 
         def nat_act(j):
-            kind, mat, a, g0, slot = items[j]
-            l32 = lpool.tile([P, 4, KP], F32)
-            if kind == "unit":
-                src = x[mat][:, a]
+            mat, rt0, nrt, g0, ng, slot = items[j]
+            l32 = npool.tile([P, 4, KP], F32)
+            if ng == 1:
+                nc.scalar.activation(
+                    out=l32[:, 0:nrt, :], in_=x[mat][:, g0, rt0 : rt0 + nrt, :], func=ACT.Ln, scale=LN_SCALE
+                )
             else:
-                src = x[mat][:, g0 : g0 + 4, a, :]
-            nc.scalar.activation(out=l32[:], in_=src, func=ACT.Ln, scale=LN_SCALE)
+                nc.scalar.activation(
+                    out=l32[:, 0:ng, :], in_=x[mat][:, g0 : g0 + ng, rt0, :], func=ACT.Ln, scale=LN_SCALE
+                )
             logs[j] = l32
 
         def nat_dve(j):
-            kind, mat, a, g0, slot = items[j]
+            mat, rt0, nrt, g0, ng, slot = items[j]
             l32 = logs[j]
-            if kind == "unit":
-                for rt in range(RT):
+            if ng == 1:
+                for i in range(nrt):
                     nc.vector.scalar_tensor_tensor(
-                        out=l32[:, rt, :], in0=l32[:, rt, :], scalar=shift[:, 0:1], in1=x[mat][:, a, rt, :],
-                        op0=ALU.subtract, op1=ALU.mult, accum_out=sp[:, mat, rt, slot : slot + 1],
+                        out=l32[:, i, :], in0=l32[:, i, :], scalar=shift[:, 0:1], in1=x[mat][:, g0, rt0 + i, :],
+                        op0=ALU.subtract, op1=ALU.mult, accum_out=sp[:, mat, rt0 + i, slot : slot + 1],
                     )
             else:
                 nc.vector.scalar_tensor_tensor(
-                    out=l32[:], in0=l32[:], scalar=shift[:, 0:1], in1=x[mat][:, g0 : g0 + 4, a, :],
-                    op0=ALU.subtract, op1=ALU.mult, accum_out=sp[:, mat, a, slot : slot + 1],
+                    out=l32[:, 0:ng, :], in0=l32[:, 0:ng, :], scalar=shift[:, 0:1],
+                    in1=x[mat][:, g0 : g0 + ng, rt0, :],
+                    op0=ALU.subtract, op1=ALU.mult, accum_out=sp[:, mat, rt0, slot : slot + 1],
                 )
 
         banks = {}
@@ -103,7 +114,9 @@ def tile_self_l1_kernel(tc, new_source, new_target, out):
         lts = {}
         pq = {}
         lq = {}
-        acc = {}
+        acc = []
+        for m in range(RT):
+            acc.append(apool.tile([P, N_ROWS], F32, tag="acc%d" % m, name="acc%d" % m))
 
         def transposes(u):
             mat, g = divmod(u, G)
@@ -123,7 +136,7 @@ def tile_self_l1_kernel(tc, new_source, new_target, out):
             for h in range(2):
                 dst = gw[:, 256 * h : 256 * h + 256, :]
                 src = banks[u][h][:].rearrange("p u r -> p r u")
-                if u >= 2 and (h == 1 or u % 4 == 0):
+                if u >= 2 and (h == 1 or u in ACT_FIRST_BANK):
                     nc.scalar.copy(out=dst, in_=src)
                 else:
                     nc.vector.tensor_copy(out=dst, in_=src)
@@ -136,22 +149,23 @@ def tile_self_l1_kernel(tc, new_source, new_target, out):
 
         def fix(u):
             gl = gpool.tile([P, 4 * N_ROWS], BF16, align_bytes=64)
-            nc.vector.tensor_scalar(
-                out=gl[:], in0=lts[u][:], scalar1=shift[:, 0:1], scalar2=None, op0=ALU.subtract
-            )
+            if u < G:
+                nc.vector.tensor_scalar(
+                    out=gl[:], in0=lts[u][:], scalar1=shift[:, 0:1], scalar2=None, op0=ALU.subtract
+                )
+            else:
+                nc.vector.tensor_scalar(
+                    out=gl[:], in0=lts[u][:], scalar1=-1.0, scalar2=shift[:, 0:1], op0=ALU.mult, op1=ALU.add
+                )
             gls[u] = gl
 
-        def quant(src, store, u):
-            codes = qpool.tile([P, N_ROWS], U32, align_bytes=64, tag="codes" + store[0], name="codes")
-            scales = qpool.tile([P, N_ROWS], U8, align_bytes=64, tag="scales" + store[0], name="scales")
+        def quant(src, kind, store, u):
+            codes = qpool.tile([P, N_ROWS], U32, align_bytes=64, tag="codes" + kind, name="codes")
+            scales = qpool.tile([P, N_ROWS], U8, align_bytes=64, tag="scales" + kind, name="scales")
             nc.vector.quantize_mx(out=codes[:].bitcast(FP8X4), scales=scales[:], in_=src[:])
-            store[1][u] = (codes, scales)
+            store[u] = (codes, scales)
 
         def passes(u):
-            mat, g = divmod(u, G)
-            if g == 0:
-                for m in range(RT):
-                    acc[m] = apool.tile([P, N_ROWS], F32, tag="acc%d" % m, name="acc%d" % m)
             pc, ps = pq[u]
             lc, ls = lq[u]
             for m in range(RT):
@@ -160,55 +174,48 @@ def tile_self_l1_kernel(tc, new_source, new_target, out):
                     out=acc[m][:],
                     lhsT=pc[:, cols].bitcast(FP8X4), lhsT_scale=ps[:, cols],
                     rhs=lc[:].bitcast(FP8X4), rhs_scale=ls[:],
-                    start=(g == 0), stop=(g == G - 1),
+                    start=(u == 0), stop=(u == UNITS - 1),
                 )
 
+        HEAD = 3
         transposes(0)
         transposes(1)
-        nat_act(0)
-        nat_act(1)
+        for j in range(HEAD):
+            nat_act(j)
         copy_out(0)
-        nat_dve(0)
-        quant(gps[0], ("p", pq), 0)
+        for j in range(HEAD - 1):
+            nat_dve(j)
+        quant(gps[0], "p", pq, 0)
         for u in range(UNITS):
             if u + 2 < UNITS:
                 transposes(u + 2)
             if u + 1 < UNITS:
                 copy_out(u + 1)
             log_t(u)
-            if u == G:
-                for m in range(RT):
-                    if m < 2:
-                        nc.vector.tensor_copy(out=cs[:, m, :], in_=acc[m][:])
-                    else:
-                        nc.scalar.copy(out=cs[:, m, :], in_=acc[m][:])
-            if u + 1 < len(items):
-                nat_dve(u + 1)
-            if u + 2 < len(items):
-                nat_act(u + 2)
+            nat_dve(HEAD - 1 + u)
+            nat_act(HEAD + u)
             fix(u)
             if u + 1 < UNITS:
-                quant(gps[u + 1], ("p", pq), u + 1)
-            quant(gls[u], ("l", lq), u)
+                quant(gps[u + 1], "p", pq, u + 1)
+            quant(gls[u], "l", lq, u)
             passes(u)
+        nat_dve(HEAD - 1 + UNITS)
 
         nc.vector.tensor_reduce(out=selfs[:], in_=sp[:], axis=AX.X, op=ALU.add)
         nc.vector.tensor_sub(out=ds[:], in0=selfs[:, 0, :], in1=selfs[:, 1, :])
-        for m in range(RT):
-            nc.vector.scalar_tensor_tensor(
-                out=xd[:, m, :], in0=acc[m][:], scalar=ds[:, m : m + 1], in1=cs[:, m, :],
-                op0=ALU.add, op1=ALU.subtract,
-            )
+        for col, m in enumerate((0, 2, 3)):
             nc.scalar.activation(
-                out=xd[:, m, :], in_=xd[:, m, :], func=ACT.Abs, accum_out=parts[:, m : m + 1]
+                out=junk_a[:], in_=acc[m][:], func=ACT.Abs, scale=-1.0, bias=ds[:, m : m + 1],
+                accum_out=parts[:, col : col + 1],
             )
-        tot = tpool.tile([P, 2, 2 * P], F32, tag="tp", name="tot")
-        nc.tensor.matmul(out=tot[:, 0, 0:RT], lhsT=ones[:], rhs=parts[:], start=True, stop=True)
-        nc.vector.tensor_reduce(out=tot1[:], in_=tot[:, 0, 0:RT], axis=AX.X, op=ALU.add)
-        nc.vector.tensor_scalar(
-            out=res[:], in0=tot1[:], scalar1=1e-4, scalar2=1.0 / (N_ROWS * N_ROWS),
-            op0=ALU.add, op1=ALU.mult,
+        nc.vector.tensor_scalar(out=xd[:], in0=acc[1][:], scalar1=ds[:, 1:2], scalar2=None, op0=ALU.subtract)
+        nc.vector.scalar_tensor_tensor(
+            out=junk_v[:], in0=xd[:], scalar=-1.0, in1=xd[:], op0=ALU.mult, op1=ALU.max,
+            accum_out=parts[:, 8:9],
         )
+        tot = tpool.tile([P, 2, 2 * P], F32, tag="tp", name="tot")
+        nc.tensor.matmul(out=tot[:, 0, 0:16], lhsT=mean_w[:], rhs=parts[:], start=True, stop=True)
+        nc.vector.tensor_reduce(out=res[:], in_=tot[:, 0, 0:16], axis=AX.X, op=ALU.add)
         dst = out
         while dst.ndim < 2:
             dst = dst.unsqueeze(0)

@@ -17,12 +17,12 @@ N_ROWS = 512
 D = 4096
 RT = N_ROWS // P
 KP = 512
+PACK = 4
 G = D // KP
 UNITS = 2 * G
 FLOPS = 2 * 2 * N_ROWS * N_ROWS * D
 
 LN_SCALE = 2.0**62
-ACT_FIRST_BANK = (3, 6, 9, 12, 15)
 
 
 def tile_self_l1_kernel(tc, new_source, new_target, out):
@@ -30,11 +30,10 @@ def tile_self_l1_kernel(tc, new_source, new_target, out):
     with ExitStack() as ctx:
         const = ctx.enter_context(tc.tile_pool(name="const", bufs=1))
         xpool = ctx.enter_context(tc.tile_pool(name="xpool", bufs=1))
-        npool = ctx.enter_context(tc.tile_pool(name="npool", bufs=4))
         lpool = ctx.enter_context(tc.tile_pool(name="lpool", bufs=3))
         gpool = ctx.enter_context(tc.tile_pool(name="gpool", bufs=3))
         qpool = ctx.enter_context(tc.tile_pool(name="qpool", bufs=3))
-        tpool = ctx.enter_context(tc.psum_pool(name="tpool", bufs=4))
+        tpool = ctx.enter_context(tc.psum_pool(name="tpool", bufs=2))
         apool = ctx.enter_context(tc.psum_pool(name="apool", bufs=1))
         ctx.enter_context(tc.manual_schedule())
 
@@ -54,12 +53,13 @@ def tile_self_l1_kernel(tc, new_source, new_target, out):
         nc.vector.memset(unit[:], 1.0)
         shift = const.tile([P, 1], F32)
         nc.scalar.activation(out=shift[:], in_=unit[:], func=ACT.Ln, scale=LN_SCALE)
+        negshift = const.tile([P, 1], F32)
+        nc.vector.tensor_scalar(out=negshift[:], in0=shift[:], scalar1=-1.0, scalar2=None, op0=ALU.mult)
         ident = const.tile([P, P], F32)
         make_identity(nc, ident[:])
         mean_w = const.tile([P, P], F32)
         nc.vector.memset(mean_w[:], 1.0 / (N_ROWS * N_ROWS))
-        sp = const.tile([P, 2, RT, 8], F32)
-        nc.vector.memset(sp[:], 0.0)
+        sp = const.tile([P, 2, RT, G], F32)
         parts = const.tile([P, 16], F32)
         nc.vector.memset(parts[:], 0.0)
         nc.vector.memset(parts[:, 15:16], 1e-4 / P)
@@ -67,46 +67,8 @@ def tile_self_l1_kernel(tc, new_source, new_target, out):
         ds = const.tile([P, RT], F32)
         junk_a = const.tile([P, N_ROWS], F32)
         xd = const.tile([P, N_ROWS], F32)
-        junk_v = const.tile([P, N_ROWS], F32)
+        junk_v = const.tile([P, PACK, P], F32)
         res = const.tile([P, 1], F32)
-
-        items = [(0, 0, 2, 0, 1, 0), (0, 2, 2, 0, 1, 0), (0, 0, 4, 1, 1, 1)]
-        for g0, slot in ((2, 2), (5, 3)):
-            for rt in range(RT):
-                items.append((0, rt, 1, g0, 3, slot))
-        for g0, slot in ((0, 0), (4, 1)):
-            for rt in range(RT):
-                items.append((1, rt, 1, g0, 4, slot))
-        logs = {}
-
-        def nat_act(j):
-            mat, rt0, nrt, g0, ng, slot = items[j]
-            l32 = npool.tile([P, 4, KP], F32)
-            if ng == 1:
-                nc.scalar.activation(
-                    out=l32[:, 0:nrt, :], in_=x[mat][:, g0, rt0 : rt0 + nrt, :], func=ACT.Ln, scale=LN_SCALE
-                )
-            else:
-                nc.scalar.activation(
-                    out=l32[:, 0:ng, :], in_=x[mat][:, g0 : g0 + ng, rt0, :], func=ACT.Ln, scale=LN_SCALE
-                )
-            logs[j] = l32
-
-        def nat_dve(j):
-            mat, rt0, nrt, g0, ng, slot = items[j]
-            l32 = logs[j]
-            if ng == 1:
-                for i in range(nrt):
-                    nc.vector.scalar_tensor_tensor(
-                        out=l32[:, i, :], in0=l32[:, i, :], scalar=shift[:, 0:1], in1=x[mat][:, g0, rt0 + i, :],
-                        op0=ALU.subtract, op1=ALU.mult, accum_out=sp[:, mat, rt0 + i, slot : slot + 1],
-                    )
-            else:
-                nc.vector.scalar_tensor_tensor(
-                    out=l32[:, 0:ng, :], in0=l32[:, 0:ng, :], scalar=shift[:, 0:1],
-                    in1=x[mat][:, g0 : g0 + ng, rt0, :],
-                    op0=ALU.subtract, op1=ALU.mult, accum_out=sp[:, mat, rt0, slot : slot + 1],
-                )
 
         banks = {}
         gps = {}
@@ -114,50 +76,58 @@ def tile_self_l1_kernel(tc, new_source, new_target, out):
         lts = {}
         pq = {}
         lq = {}
+        back = {}
         acc = []
         for m in range(RT):
             acc.append(apool.tile([P, N_ROWS], F32, tag="acc%d" % m, name="acc%d" % m))
 
-        def transposes(u):
+        def transposes(u, h):
             mat, g = divmod(u, G)
-            pair = []
-            for h in range(2):
-                tp = tpool.tile([P, 2, 2 * P], F32)
-                for j in range(2):
-                    words = x[mat][:, g, 2 * h + j, :].bitcast(F32).rearrange("p (w u) -> p w u", u=2)
-                    for uu in range(2):
-                        nc.tensor.transpose(tp[:, uu, P * j : P * j + P], words[:, :, uu], ident[:])
-                pair.append(tp)
-            banks[u] = pair
+            tp = tpool.tile([P, 2, 2 * P], F32)
+            for j in range(2):
+                words = x[mat][:, g, 2 * h + j, :].bitcast(F32).rearrange("p (w u) -> p w u", u=2)
+                for uu in range(2):
+                    nc.tensor.transpose(tp[:, uu, P * j : P * j + P], words[:, :, uu], ident[:])
+            banks[(u, h)] = tp
 
         def copy_out(u):
-            gp = gpool.tile([P, 4 * N_ROWS], BF16, align_bytes=64)
+            gp = gpool.tile([P, PACK * N_ROWS], BF16, align_bytes=64)
             gw = gp[:].bitcast(F32).rearrange("p (r u) -> p r u", u=2)
             for h in range(2):
-                dst = gw[:, 256 * h : 256 * h + 256, :]
-                src = banks[u][h][:].rearrange("p u r -> p r u")
-                if u >= 2 and (h == 1 or u in ACT_FIRST_BANK):
-                    nc.scalar.copy(out=dst, in_=src)
-                else:
-                    nc.vector.tensor_copy(out=dst, in_=src)
+                nc.scalar.copy(
+                    out=gw[:, 256 * h : 256 * h + 256, :], in_=banks[(u, h)][:].rearrange("p u r -> p r u")
+                )
             gps[u] = gp
 
         def log_t(u):
-            lt = lpool.tile([P, 4 * N_ROWS], F32)
-            nc.scalar.activation(out=lt[:], in_=gps[u][:], func=ACT.Ln, scale=LN_SCALE)
+            lt = lpool.tile([P, PACK, N_ROWS], F32)
+            nc.scalar.activation(
+                out=lt[:], in_=gps[u][:].rearrange("p (r t) -> p t r", t=PACK), func=ACT.Ln, scale=LN_SCALE
+            )
             lts[u] = lt
 
         def fix(u):
-            gl = gpool.tile([P, 4 * N_ROWS], BF16, align_bytes=64)
-            if u < G:
-                nc.vector.tensor_scalar(
-                    out=gl[:], in0=lts[u][:], scalar1=shift[:, 0:1], scalar2=None, op0=ALU.subtract
-                )
-            else:
-                nc.vector.tensor_scalar(
-                    out=gl[:], in0=lts[u][:], scalar1=-1.0, scalar2=shift[:, 0:1], op0=ALU.mult, op1=ALU.add
-                )
+            gl = gpool.tile([P, PACK * N_ROWS], BF16, align_bytes=64)
+            sign, off = (1.0, negshift) if u < G else (-1.0, shift)
+            nc.gpsimd.tensor_scalar(
+                out=gl[:].rearrange("p (r t) -> p r t", t=PACK), in0=lts[u][:].rearrange("p t r -> p r t"),
+                scalar1=sign, scalar2=off[:, 0:1], op0=ALU.mult, op1=ALU.add,
+            )
             gls[u] = gl
+
+        def back_t(u, rt):
+            bk = tpool.tile([P, PACK, P], F32)
+            for t in range(PACK):
+                nc.tensor.transpose(bk[:, t, :], lts[u][:, t, P * rt : P * rt + P], ident[:])
+            back[(u, rt)] = bk
+
+        def self_part(u, rt):
+            mat, g = divmod(u, G)
+            nc.vector.scalar_tensor_tensor(
+                out=junk_v[:], in0=back[(u, rt)][:], scalar=shift[:, 0:1],
+                in1=x[mat][:, g, rt, :].rearrange("p (q t) -> p t q", t=PACK),
+                op0=ALU.subtract, op1=ALU.mult, accum_out=sp[:, mat, rt, g : g + 1],
+            )
 
         def quant(src, kind, store, u):
             codes = qpool.tile([P, N_ROWS], U32, align_bytes=64, tag="codes" + kind, name="codes")
@@ -177,29 +147,37 @@ def tile_self_l1_kernel(tc, new_source, new_target, out):
                     start=(u == 0), stop=(u == UNITS - 1),
                 )
 
-        HEAD = 3
-        transposes(0)
-        transposes(1)
-        for j in range(HEAD):
-            nat_act(j)
+        transposes(0, 0)
+        transposes(0, 1)
         copy_out(0)
-        for j in range(HEAD - 1):
-            nat_dve(j)
+        transposes(1, 0)
+        transposes(1, 1)
+        log_t(0)
         quant(gps[0], "p", pq, 0)
         for u in range(UNITS):
-            if u + 2 < UNITS:
-                transposes(u + 2)
             if u + 1 < UNITS:
                 copy_out(u + 1)
-            log_t(u)
-            nat_dve(HEAD - 1 + u)
-            nat_act(HEAD + u)
+            back_t(u, 0)
+            back_t(u, 1)
+            self_part(u, 0)
+            self_part(u, 1)
+            if u + 2 < UNITS:
+                transposes(u + 2, 0)
+            back_t(u, 2)
+            self_part(u, 2)
+            if u + 2 < UNITS:
+                transposes(u + 2, 1)
+            back_t(u, 3)
+            self_part(u, 3)
             fix(u)
             if u + 1 < UNITS:
-                quant(gps[u + 1], "p", pq, u + 1)
+                log_t(u + 1)
             quant(gls[u], "l", lq, u)
-            passes(u)
-        nat_dve(HEAD - 1 + UNITS)
+            if u + 1 < UNITS:
+                quant(gps[u + 1], "p", pq, u + 1)
+            if u >= 1:
+                passes(u - 1)
+        passes(UNITS - 1)
 
         nc.vector.tensor_reduce(out=selfs[:], in_=sp[:], axis=AX.X, op=ALU.add)
         nc.vector.tensor_sub(out=ds[:], in0=selfs[:, 0, :], in1=selfs[:, 1, :])
@@ -210,7 +188,7 @@ def tile_self_l1_kernel(tc, new_source, new_target, out):
             )
         nc.vector.tensor_scalar(out=xd[:], in0=acc[1][:], scalar1=ds[:, 1:2], scalar2=None, op0=ALU.subtract)
         nc.vector.scalar_tensor_tensor(
-            out=junk_v[:], in0=xd[:], scalar=-1.0, in1=xd[:], op0=ALU.mult, op1=ALU.max,
+            out=junk_v[:].rearrange("p t q -> p (t q)"), in0=xd[:], scalar=-1.0, in1=xd[:], op0=ALU.mult, op1=ALU.max,
             accum_out=parts[:, 8:9],
         )
         tot = tpool.tile([P, 2, 2 * P], F32, tag="tp", name="tot")

@@ -135,10 +135,10 @@ def tile_self_l1_kernel(tc, new_source, new_target, out):
             nc.vector.quantize_mx(out=codes[:].bitcast(FP8X4), scales=scales[:], in_=src[:])
             store[u] = (codes, scales)
 
-        def passes(u):
+        def passes(u, tiles):
             pc, ps = pq[u]
             lc, ls = lq[u]
-            for m in range(RT):
+            for m in tiles:
                 cols = slice(P * m, P * m + P)
                 nc.tensor.matmul_mx(
                     out=acc[m][:],
@@ -161,14 +161,15 @@ def tile_self_l1_kernel(tc, new_source, new_target, out):
             back_t(u, 1)
             self_part(u, 0)
             self_part(u, 1)
-            if u + 2 < UNITS:
-                transposes(u + 2, 0)
+            if u >= 1:
+                passes(u - 1, (0, 1))
             back_t(u, 2)
             self_part(u, 2)
-            if u + 2 < UNITS:
-                transposes(u + 2, 1)
             back_t(u, 3)
             self_part(u, 3)
+            if u + 2 < UNITS:
+                transposes(u + 2, 0)
+                transposes(u + 2, 1)
             fix(u)
             if u + 1 < UNITS:
                 log_t(u + 1)
@@ -176,8 +177,8 @@ def tile_self_l1_kernel(tc, new_source, new_target, out):
             if u + 1 < UNITS:
                 quant(gps[u + 1], "p", pq, u + 1)
             if u >= 1:
-                passes(u - 1)
-        passes(UNITS - 1)
+                passes(u - 1, (2, 3))
+        passes(UNITS - 1, (0, 1, 2, 3))
 
         nc.vector.tensor_reduce(out=selfs[:], in_=sp[:], axis=AX.X, op=ALU.add)
         nc.vector.tensor_sub(out=ds[:], in0=selfs[:, 0, :], in1=selfs[:, 1, :])

@@ -17,12 +17,12 @@ N_ROWS = 512
 D = 4096
 RT = N_ROWS // P
 KP = 512
-PACK = 4
 G = D // KP
 UNITS = 2 * G
 FLOPS = 2 * 2 * N_ROWS * N_ROWS * D
 
 LN_SCALE = 2.0**62
+ACT_FIRST_BANK = (3, 6, 9, 12, 15)
 
 
 def tile_self_l1_kernel(tc, new_source, new_target, out):
@@ -30,10 +30,11 @@ def tile_self_l1_kernel(tc, new_source, new_target, out):
     with ExitStack() as ctx:
         const = ctx.enter_context(tc.tile_pool(name="const", bufs=1))
         xpool = ctx.enter_context(tc.tile_pool(name="xpool", bufs=1))
+        npool = ctx.enter_context(tc.tile_pool(name="npool", bufs=4))
         lpool = ctx.enter_context(tc.tile_pool(name="lpool", bufs=3))
         gpool = ctx.enter_context(tc.tile_pool(name="gpool", bufs=3))
         qpool = ctx.enter_context(tc.tile_pool(name="qpool", bufs=3))
-        tpool = ctx.enter_context(tc.psum_pool(name="tpool", bufs=2))
+        tpool = ctx.enter_context(tc.psum_pool(name="tpool", bufs=4))
         apool = ctx.enter_context(tc.psum_pool(name="apool", bufs=1))
         ctx.enter_context(tc.manual_schedule())
 
@@ -53,22 +54,60 @@ def tile_self_l1_kernel(tc, new_source, new_target, out):
         nc.vector.memset(unit[:], 1.0)
         shift = const.tile([P, 1], F32)
         nc.scalar.activation(out=shift[:], in_=unit[:], func=ACT.Ln, scale=LN_SCALE)
-        negshift = const.tile([P, 1], F32)
-        nc.vector.tensor_scalar(out=negshift[:], in0=shift[:], scalar1=-1.0, scalar2=None, op0=ALU.mult)
         ident = const.tile([P, P], F32)
         make_identity(nc, ident[:])
         mean_w = const.tile([P, P], F32)
         nc.vector.memset(mean_w[:], 1.0 / (N_ROWS * N_ROWS))
-        sp = const.tile([P, 2, RT, G], F32)
+        sp = const.tile([P, 2, RT, 8], F32)
+        nc.vector.memset(sp[:], 0.0)
         parts = const.tile([P, 16], F32)
         nc.vector.memset(parts[:], 0.0)
         nc.vector.memset(parts[:, 15:16], 1e-4 / P)
         selfs = const.tile([P, 2, RT], F32)
         ds = const.tile([P, RT], F32)
+        ds3 = const.tile([P, 1], F32)
         junk_a = const.tile([P, N_ROWS], F32)
         xd = const.tile([P, N_ROWS], F32)
-        junk_v = const.tile([P, PACK, P], F32)
+        junk_v = const.tile([P, N_ROWS], F32)
         res = const.tile([P, 1], F32)
+
+        items = [(0, 0, 2, 0, 1, 0), (0, 2, 2, 0, 1, 0), (0, 0, 4, 1, 1, 1)]
+        for g0, slot in ((2, 2), (5, 3)):
+            for rt in range(RT):
+                items.append((0, rt, 1, g0, 3, slot))
+        for g0, slot in ((0, 0), (4, 1)):
+            for rt in range(RT):
+                items.append((1, rt, 1, g0, 4, slot))
+        logs = {}
+
+        def nat_act(j):
+            mat, rt0, nrt, g0, ng, slot = items[j]
+            l32 = npool.tile([P, 4, KP], F32)
+            if ng == 1:
+                nc.scalar.activation(
+                    out=l32[:, 0:nrt, :], in_=x[mat][:, g0, rt0 : rt0 + nrt, :], func=ACT.Ln, scale=LN_SCALE
+                )
+            else:
+                nc.scalar.activation(
+                    out=l32[:, 0:ng, :], in_=x[mat][:, g0 : g0 + ng, rt0, :], func=ACT.Ln, scale=LN_SCALE
+                )
+            logs[j] = l32
+
+        def nat_dve(j):
+            mat, rt0, nrt, g0, ng, slot = items[j]
+            l32 = logs[j]
+            if ng == 1:
+                for i in range(nrt):
+                    nc.vector.scalar_tensor_tensor(
+                        out=l32[:, i, :], in0=l32[:, i, :], scalar=shift[:, 0:1], in1=x[mat][:, g0, rt0 + i, :],
+                        op0=ALU.subtract, op1=ALU.mult, accum_out=sp[:, mat, rt0 + i, slot : slot + 1],
+                    )
+            else:
+                nc.vector.scalar_tensor_tensor(
+                    out=l32[:, 0:ng, :], in0=l32[:, 0:ng, :], scalar=shift[:, 0:1],
+                    in1=x[mat][:, g0 : g0 + ng, rt0, :],
+                    op0=ALU.subtract, op1=ALU.mult, accum_out=sp[:, mat, rt0, slot : slot + 1],
+                )
 
         banks = {}
         gps = {}
@@ -76,58 +115,50 @@ def tile_self_l1_kernel(tc, new_source, new_target, out):
         lts = {}
         pq = {}
         lq = {}
-        back = {}
         acc = []
         for m in range(RT):
             acc.append(apool.tile([P, N_ROWS], F32, tag="acc%d" % m, name="acc%d" % m))
 
-        def transposes(u, h):
+        def transposes(u):
             mat, g = divmod(u, G)
-            tp = tpool.tile([P, 2, 2 * P], F32)
-            for j in range(2):
-                words = x[mat][:, g, 2 * h + j, :].bitcast(F32).rearrange("p (w u) -> p w u", u=2)
-                for uu in range(2):
-                    nc.tensor.transpose(tp[:, uu, P * j : P * j + P], words[:, :, uu], ident[:])
-            banks[(u, h)] = tp
+            pair = []
+            for h in range(2):
+                tp = tpool.tile([P, 2, 2 * P], F32)
+                for j in range(2):
+                    words = x[mat][:, g, 2 * h + j, :].bitcast(F32).rearrange("p (w u) -> p w u", u=2)
+                    for uu in range(2):
+                        nc.tensor.transpose(tp[:, uu, P * j : P * j + P], words[:, :, uu], ident[:])
+                pair.append(tp)
+            banks[u] = pair
 
         def copy_out(u):
-            gp = gpool.tile([P, PACK * N_ROWS], BF16, align_bytes=64)
+            gp = gpool.tile([P, 4 * N_ROWS], BF16, align_bytes=64)
             gw = gp[:].bitcast(F32).rearrange("p (r u) -> p r u", u=2)
             for h in range(2):
-                nc.scalar.copy(
-                    out=gw[:, 256 * h : 256 * h + 256, :], in_=banks[(u, h)][:].rearrange("p u r -> p r u")
-                )
+                dst = gw[:, 256 * h : 256 * h + 256, :]
+                src = banks[u][h][:].rearrange("p u r -> p r u")
+                if u >= 2 and (h == 1 or u in ACT_FIRST_BANK):
+                    nc.scalar.copy(out=dst, in_=src)
+                else:
+                    nc.vector.tensor_copy(out=dst, in_=src)
             gps[u] = gp
 
         def log_t(u):
-            lt = lpool.tile([P, PACK, N_ROWS], F32)
-            nc.scalar.activation(
-                out=lt[:], in_=gps[u][:].rearrange("p (r t) -> p t r", t=PACK), func=ACT.Ln, scale=LN_SCALE
-            )
+            lt = lpool.tile([P, 4 * N_ROWS], F32)
+            nc.scalar.activation(out=lt[:], in_=gps[u][:], func=ACT.Ln, scale=LN_SCALE)
             lts[u] = lt
 
         def fix(u):
-            gl = gpool.tile([P, PACK * N_ROWS], BF16, align_bytes=64)
-            sign, off = (1.0, negshift) if u < G else (-1.0, shift)
-            nc.gpsimd.tensor_scalar(
-                out=gl[:].rearrange("p (r t) -> p r t", t=PACK), in0=lts[u][:].rearrange("p t r -> p r t"),
-                scalar1=sign, scalar2=off[:, 0:1], op0=ALU.mult, op1=ALU.add,
-            )
+            gl = gpool.tile([P, 4 * N_ROWS], BF16, align_bytes=64)
+            if u < G:
+                nc.vector.tensor_scalar(
+                    out=gl[:], in0=lts[u][:], scalar1=shift[:, 0:1], scalar2=None, op0=ALU.subtract
+                )
+            else:
+                nc.vector.tensor_scalar(
+                    out=gl[:], in0=lts[u][:], scalar1=-1.0, scalar2=shift[:, 0:1], op0=ALU.mult, op1=ALU.add
+                )
             gls[u] = gl
-
-        def back_t(u, rt):
-            bk = tpool.tile([P, PACK, P], F32)
-            for t in range(PACK):
-                nc.tensor.transpose(bk[:, t, :], lts[u][:, t, P * rt : P * rt + P], ident[:])
-            back[(u, rt)] = bk
-
-        def self_part(u, rt):
-            mat, g = divmod(u, G)
-            nc.vector.scalar_tensor_tensor(
-                out=junk_v[:], in0=back[(u, rt)][:], scalar=shift[:, 0:1],
-                in1=x[mat][:, g, rt, :].rearrange("p (q t) -> p t q", t=PACK),
-                op0=ALU.subtract, op1=ALU.mult, accum_out=sp[:, mat, rt, g : g + 1],
-            )
 
         def quant(src, kind, store, u):
             codes = qpool.tile([P, N_ROWS], U32, align_bytes=64, tag="codes" + kind, name="codes")
@@ -135,10 +166,10 @@ def tile_self_l1_kernel(tc, new_source, new_target, out):
             nc.vector.quantize_mx(out=codes[:].bitcast(FP8X4), scales=scales[:], in_=src[:])
             store[u] = (codes, scales)
 
-        def passes(u, tiles):
+        def passes(u):
             pc, ps = pq[u]
             lc, ls = lq[u]
-            for m in tiles:
+            for m in range(RT):
                 cols = slice(P * m, P * m + P)
                 nc.tensor.matmul_mx(
                     out=acc[m][:],
@@ -147,49 +178,47 @@ def tile_self_l1_kernel(tc, new_source, new_target, out):
                     start=(u == 0), stop=(u == UNITS - 1),
                 )
 
-        transposes(0, 0)
-        transposes(0, 1)
+        HEAD = 3
+        transposes(0)
+        transposes(1)
+        for j in range(HEAD):
+            nat_act(j)
         copy_out(0)
-        transposes(1, 0)
-        transposes(1, 1)
-        log_t(0)
+        for j in range(HEAD - 1):
+            nat_dve(j)
         quant(gps[0], "p", pq, 0)
         for u in range(UNITS):
+            if u + 2 < UNITS:
+                transposes(u + 2)
+            if u >= 1:
+                fix(u - 1)
             if u + 1 < UNITS:
                 copy_out(u + 1)
-            back_t(u, 0)
-            back_t(u, 1)
-            self_part(u, 0)
-            self_part(u, 1)
+            log_t(u)
             if u >= 1:
-                passes(u - 1, (0, 1))
-            back_t(u, 2)
-            self_part(u, 2)
-            back_t(u, 3)
-            self_part(u, 3)
-            if u + 2 < UNITS:
-                transposes(u + 2, 0)
-                transposes(u + 2, 1)
-            fix(u)
-            if u + 1 < UNITS:
-                log_t(u + 1)
-            quant(gls[u], "l", lq, u)
+                quant(gls[u - 1], "l", lq, u - 1)
+                passes(u - 1)
+            nat_dve(HEAD - 1 + u)
+            nat_act(HEAD + u)
             if u + 1 < UNITS:
                 quant(gps[u + 1], "p", pq, u + 1)
-            if u >= 1:
-                passes(u - 1, (2, 3))
-        passes(UNITS - 1, (0, 1, 2, 3))
-
+        last = UNITS - 1
+        fix(last)
         nc.vector.tensor_reduce(out=selfs[:], in_=sp[:], axis=AX.X, op=ALU.add)
         nc.vector.tensor_sub(out=ds[:], in0=selfs[:, 0, :], in1=selfs[:, 1, :])
+        quant(gls[last], "l", lq, last)
+        passes(last)
+        nat_dve(HEAD - 1 + UNITS)
+        nc.vector.tensor_sub(out=ds3[:], in0=ds[:, 3:4], in1=sp[:, 1, 3, 1:2])
         for col, m in enumerate((0, 2, 3)):
             nc.scalar.activation(
-                out=junk_a[:], in_=acc[m][:], func=ACT.Abs, scale=-1.0, bias=ds[:, m : m + 1],
+                out=junk_a[:], in_=acc[m][:], func=ACT.Abs, scale=-1.0,
+                bias=(ds3[:, 0:1] if m == 3 else ds[:, m : m + 1]),
                 accum_out=parts[:, col : col + 1],
             )
         nc.vector.tensor_scalar(out=xd[:], in0=acc[1][:], scalar1=ds[:, 1:2], scalar2=None, op0=ALU.subtract)
         nc.vector.scalar_tensor_tensor(
-            out=junk_v[:].rearrange("p t q -> p (t q)"), in0=xd[:], scalar=-1.0, in1=xd[:], op0=ALU.mult, op1=ALU.max,
+            out=junk_v[:], in0=xd[:], scalar=-1.0, in1=xd[:], op0=ALU.mult, op1=ALU.max,
             accum_out=parts[:, 8:9],
         )
         tot = tpool.tile([P, 2, 2 * P], F32, tag="tp", name="tot")

@@ -36,7 +36,6 @@ def tile_self_l1_kernel(tc, new_source, new_target, out):
         qpool = ctx.enter_context(tc.tile_pool(name="qpool", bufs=3))
         tpool = ctx.enter_context(tc.psum_pool(name="tpool", bufs=4))
         apool = ctx.enter_context(tc.psum_pool(name="apool", bufs=1))
-        ctx.enter_context(tc.manual_schedule())
 
         x_src = xpool.tile([P, G, RT, KP], BF16)
         x_tgt = xpool.tile([P, G, RT, KP], BF16)

@@ -22,7 +22,7 @@ UNITS = 2 * G
 FLOPS = 2 * 2 * N_ROWS * N_ROWS * D
 
 LN_SCALE = 2.0**62
-ACT_FIRST_BANK = (3, 6, 9, 12, 15)
+ACT_FIRST_BANK = (3, 5, 7, 9, 11, 13, 15)
 
 
 def tile_self_l1_kernel(tc, new_source, new_target, out):
@@ -36,6 +36,7 @@ def tile_self_l1_kernel(tc, new_source, new_target, out):
         qpool = ctx.enter_context(tc.tile_pool(name="qpool", bufs=3))
         tpool = ctx.enter_context(tc.psum_pool(name="tpool", bufs=4))
         apool = ctx.enter_context(tc.psum_pool(name="apool", bufs=1))
+        ctx.enter_context(tc.manual_schedule())
 
         x_src = xpool.tile([P, G, RT, KP], BF16)
         x_tgt = xpool.tile([P, G, RT, KP], BF16)

@@ -22,7 +22,7 @@ UNITS = 2 * G
 FLOPS = 2 * 2 * N_ROWS * N_ROWS * D
 
 LN_SCALE = 2.0**62
-ACT_FIRST_BANK = (3, 5, 7, 9, 11, 13, 15)
+GROUPS = ((0,), (1,), (2, 3), (4, 5), (6, 7), (8, 9), (10, 11), (12, 13), (14,), (15,))
 
 
 def tile_self_l1_kernel(tc, new_source, new_target, out):
@@ -31,10 +31,10 @@ def tile_self_l1_kernel(tc, new_source, new_target, out):
         const = ctx.enter_context(tc.tile_pool(name="const", bufs=1))
         xpool = ctx.enter_context(tc.tile_pool(name="xpool", bufs=1))
         npool = ctx.enter_context(tc.tile_pool(name="npool", bufs=4))
-        lpool = ctx.enter_context(tc.tile_pool(name="lpool", bufs=3))
+        rpool = ctx.enter_context(tc.tile_pool(name="rpool", bufs=3))
         gpool = ctx.enter_context(tc.tile_pool(name="gpool", bufs=3))
         qpool = ctx.enter_context(tc.tile_pool(name="qpool", bufs=3))
-        tpool = ctx.enter_context(tc.psum_pool(name="tpool", bufs=4))
+        tpool = ctx.enter_context(tc.psum_pool(name="tpool", bufs=2))
         apool = ctx.enter_context(tc.psum_pool(name="apool", bufs=1))
         ctx.enter_context(tc.manual_schedule())
 
@@ -65,100 +65,88 @@ def tile_self_l1_kernel(tc, new_source, new_target, out):
         nc.vector.memset(parts[:, 15:16], 1e-4 / P)
         selfs = const.tile([P, 2, RT], F32)
         ds = const.tile([P, RT], F32)
-        ds3 = const.tile([P, 1], F32)
         junk_a = const.tile([P, N_ROWS], F32)
         xd = const.tile([P, N_ROWS], F32)
         junk_v = const.tile([P, N_ROWS], F32)
         res = const.tile([P, 1], F32)
 
-        items = [(0, 0, 2, 0, 1, 0), (0, 2, 2, 0, 1, 0), (0, 0, 4, 1, 1, 1)]
-        for g0, slot in ((2, 2), (5, 3)):
-            for rt in range(RT):
-                items.append((0, rt, 1, g0, 3, slot))
-        for g0, slot in ((0, 0), (4, 1)):
-            for rt in range(RT):
-                items.append((1, rt, 1, g0, 4, slot))
+        group_of = {}
+        for k, units in enumerate(GROUPS):
+            for i, u in enumerate(units):
+                group_of[u] = (k, i)
         logs = {}
-
-        def nat_act(j):
-            mat, rt0, nrt, g0, ng, slot = items[j]
-            l32 = npool.tile([P, 4, KP], F32)
-            if ng == 1:
-                nc.scalar.activation(
-                    out=l32[:, 0:nrt, :], in_=x[mat][:, g0, rt0 : rt0 + nrt, :], func=ACT.Ln, scale=LN_SCALE
-                )
-            else:
-                nc.scalar.activation(
-                    out=l32[:, 0:ng, :], in_=x[mat][:, g0 : g0 + ng, rt0, :], func=ACT.Ln, scale=LN_SCALE
-                )
-            logs[j] = l32
-
-        def nat_dve(j):
-            mat, rt0, nrt, g0, ng, slot = items[j]
-            l32 = logs[j]
-            if ng == 1:
-                for i in range(nrt):
-                    nc.vector.scalar_tensor_tensor(
-                        out=l32[:, i, :], in0=l32[:, i, :], scalar=shift[:, 0:1], in1=x[mat][:, g0, rt0 + i, :],
-                        op0=ALU.subtract, op1=ALU.mult, accum_out=sp[:, mat, rt0 + i, slot : slot + 1],
-                    )
-            else:
-                nc.vector.scalar_tensor_tensor(
-                    out=l32[:, 0:ng, :], in0=l32[:, 0:ng, :], scalar=shift[:, 0:1],
-                    in1=x[mat][:, g0 : g0 + ng, rt0, :],
-                    op0=ALU.subtract, op1=ALU.mult, accum_out=sp[:, mat, rt0, slot : slot + 1],
-                )
-
+        rounded = {}
         banks = {}
         gps = {}
         gls = {}
-        lts = {}
         pq = {}
         lq = {}
         acc = []
         for m in range(RT):
             acc.append(apool.tile([P, N_ROWS], F32, tag="acc%d" % m, name="acc%d" % m))
 
-        def transposes(u):
+        def log_rows(u):
             mat, g = divmod(u, G)
-            pair = []
-            for h in range(2):
-                tp = tpool.tile([P, 2, 2 * P], F32)
-                for j in range(2):
-                    words = x[mat][:, g, 2 * h + j, :].bitcast(F32).rearrange("p (w u) -> p w u", u=2)
-                    for uu in range(2):
-                        nc.tensor.transpose(tp[:, uu, P * j : P * j + P], words[:, :, uu], ident[:])
-                pair.append(tp)
-            banks[u] = pair
+            k, i = group_of[u]
+            if i == 0:
+                l32 = npool.tile([P, 2, RT, KP], F32, name="l32")
+                logs[k] = l32
+            l32 = logs[k]
+            if u == 0:
+                for h in range(2):
+                    rows = slice(2 * h, 2 * h + 2)
+                    nc.scalar.activation(
+                        out=l32[:, i, rows], in_=x[mat][:, g, rows], func=ACT.Ln, scale=LN_SCALE
+                    )
+            else:
+                nc.scalar.activation(out=l32[:, i], in_=x[mat][:, g], func=ACT.Ln, scale=LN_SCALE)
 
-        def copy_out(u):
-            gp = gpool.tile([P, 4 * N_ROWS], BF16, align_bytes=64)
-            gw = gp[:].bitcast(F32).rearrange("p (r u) -> p r u", u=2)
-            for h in range(2):
-                dst = gw[:, 256 * h : 256 * h + 256, :]
-                src = banks[u][h][:].rearrange("p u r -> p r u")
-                if u >= 2 and (h == 1 or u in ACT_FIRST_BANK):
-                    nc.scalar.copy(out=dst, in_=src)
-                else:
-                    nc.vector.tensor_copy(out=dst, in_=src)
-            gps[u] = gp
-
-        def log_t(u):
-            lt = lpool.tile([P, 4 * N_ROWS], F32)
-            nc.scalar.activation(out=lt[:], in_=gps[u][:], func=ACT.Ln, scale=LN_SCALE)
-            lts[u] = lt
-
-        def fix(u):
-            gl = gpool.tile([P, 4 * N_ROWS], BF16, align_bytes=64)
+        def round_rows(u):
+            k, i = group_of[u]
+            r16 = rpool.tile([P, RT, KP], BF16, name="r16")
             if u < G:
                 nc.vector.tensor_scalar(
-                    out=gl[:], in0=lts[u][:], scalar1=shift[:, 0:1], scalar2=None, op0=ALU.subtract
+                    out=r16[:], in0=logs[k][:, i], scalar1=shift[:, 0:1], scalar2=None, op0=ALU.subtract
                 )
             else:
                 nc.vector.tensor_scalar(
-                    out=gl[:], in0=lts[u][:], scalar1=-1.0, scalar2=shift[:, 0:1], op0=ALU.mult, op1=ALU.add
+                    out=r16[:], in0=logs[k][:, i], scalar1=-1.0, scalar2=shift[:, 0:1], op0=ALU.mult, op1=ALU.add
                 )
-            gls[u] = gl
+            rounded[u] = r16
+
+        def self_term(k, rt):
+            units = GROUPS[k]
+            mat, g0 = divmod(units[0], G)
+            n = len(units)
+            l32 = logs[k]
+            nc.vector.scalar_tensor_tensor(
+                out=l32[:, 0:n, rt, :], in0=l32[:, 0:n, rt, :], scalar=shift[:, 0:1],
+                in1=x[mat][:, g0 : g0 + n, rt, :],
+                op0=ALU.subtract, op1=ALU.mult, accum_out=sp[:, mat, rt, k % 5 : k % 5 + 1],
+            )
+
+        def transposes(src, kind, u):
+            pair = []
+            for h in range(2):
+                tp = tpool.tile([P, 2, 2 * P], F32, tag="tp" + kind, name="tp")
+                for j in range(2):
+                    words = src[:, 2 * h + j, :].bitcast(F32).rearrange("p (w u) -> p w u", u=2)
+                    for uu in range(2):
+                        nc.tensor.transpose(tp[:, uu, P * j : P * j + P], words[:, :, uu], ident[:])
+                pair.append(tp)
+            banks[kind, u] = pair
+
+        def copy_out(kind, u, vector=False):
+            gp = gpool.tile([P, 4 * N_ROWS], BF16, align_bytes=64, tag="g" + kind, name="gp")
+            gw = gp[:].bitcast(F32).rearrange("p (r u) -> p r u", u=2)
+            for h in range(2):
+                dst = gw[:, 256 * h : 256 * h + 256, :]
+                src = banks[kind, u][h][:].rearrange("p u r -> p r u")
+                if vector:
+                    nc.vector.tensor_copy(out=dst, in_=src)
+                else:
+                    nc.scalar.copy(out=dst, in_=src)
+            (gps if kind == "p" else gls)[u] = gp
 
         def quant(src, kind, store, u):
             codes = qpool.tile([P, N_ROWS], U32, align_bytes=64, tag="codes" + kind, name="codes")
@@ -178,42 +166,47 @@ def tile_self_l1_kernel(tc, new_source, new_target, out):
                     start=(u == 0), stop=(u == UNITS - 1),
                 )
 
-        HEAD = 3
-        transposes(0)
-        transposes(1)
-        for j in range(HEAD):
-            nat_act(j)
-        copy_out(0)
-        for j in range(HEAD - 1):
-            nat_dve(j)
-        quant(gps[0], "p", pq, 0)
+        waiting = []
+        transposes(x[0][:, 0], "p", 0)
+        log_rows(0)
+        copy_out("p", 0, vector=True)
         for u in range(UNITS):
-            if u + 2 < UNITS:
-                transposes(u + 2)
-            if u >= 1:
-                fix(u - 1)
+            mat, g = divmod(u + 1, G)
+            round_rows(u)
             if u + 1 < UNITS:
-                copy_out(u + 1)
-            log_t(u)
+                transposes(x[mat][:, g], "p", u + 1)
+            transposes(rounded[u], "l", u)
+            if u + 1 < UNITS:
+                log_rows(u + 1)
             if u >= 1:
                 quant(gls[u - 1], "l", lq, u - 1)
+            quant(gps[u], "p", pq, u)
+            if u >= 1:
                 passes(u - 1)
-            nat_dve(HEAD - 1 + u)
-            nat_act(HEAD + u)
+            k, i = group_of[u]
+            n = len(GROUPS[k])
+            if i == n - 1 and u < UNITS - 1:
+                waiting += [(k, rt, n) for rt in range(RT)]
+            done = 0
+            while waiting and done < 4:
+                k, rt, n = waiting.pop(0)
+                self_term(k, rt)
+                done += n
             if u + 1 < UNITS:
-                quant(gps[u + 1], "p", pq, u + 1)
+                copy_out("p", u + 1)
+            copy_out("l", u)
         last = UNITS - 1
-        fix(last)
-        nc.vector.tensor_reduce(out=selfs[:], in_=sp[:], axis=AX.X, op=ALU.add)
-        nc.vector.tensor_sub(out=ds[:], in0=selfs[:, 0, :], in1=selfs[:, 1, :])
+        for k, rt, n in waiting:
+            self_term(k, rt)
         quant(gls[last], "l", lq, last)
         passes(last)
-        nat_dve(HEAD - 1 + UNITS)
-        nc.vector.tensor_sub(out=ds3[:], in0=ds[:, 3:4], in1=sp[:, 1, 3, 1:2])
+        for rt in range(RT):
+            self_term(len(GROUPS) - 1, rt)
+        nc.vector.tensor_reduce(out=selfs[:], in_=sp[:], axis=AX.X, op=ALU.add)
+        nc.vector.tensor_sub(out=ds[:], in0=selfs[:, 0, :], in1=selfs[:, 1, :])
         for col, m in enumerate((0, 2, 3)):
             nc.scalar.activation(
-                out=junk_a[:], in_=acc[m][:], func=ACT.Abs, scale=-1.0,
-                bias=(ds3[:, 0:1] if m == 3 else ds[:, m : m + 1]),
+                out=junk_a[:], in_=acc[m][:], func=ACT.Abs, scale=-1.0, bias=ds[:, m : m + 1],
                 accum_out=parts[:, col : col + 1],
             )
         nc.vector.tensor_scalar(out=xd[:], in0=acc[1][:], scalar1=ds[:, 1:2], scalar2=None, op0=ALU.subtract)
@@ -221,7 +214,7 @@ def tile_self_l1_kernel(tc, new_source, new_target, out):
             out=junk_v[:], in0=xd[:], scalar=-1.0, in1=xd[:], op0=ALU.mult, op1=ALU.max,
             accum_out=parts[:, 8:9],
         )
-        tot = tpool.tile([P, 2, 2 * P], F32, tag="tp", name="tot")
+        tot = tpool.tile([P, 2, 2 * P], F32, tag="tpp", name="tot")
         nc.tensor.matmul(out=tot[:, 0, 0:16], lhsT=mean_w[:], rhs=parts[:], start=True, stop=True)
         nc.vector.tensor_reduce(out=res[:], in_=tot[:, 0, 0:16], axis=AX.X, op=ALU.add)
         dst = out

@@ -103,16 +103,24 @@ def tile_self_l1_kernel(tc, new_source, new_target, out):
 
         def round_rows(u):
             k, i = group_of[u]
-            r16 = rpool.tile([P, RT, KP], BF16, name="r16")
+            r16 = rpool.tile([P, 2, RT * P, 2], BF16, name="r16")
+            src = logs[k][:, i].rearrange("p rt (d u e) -> p u (rt d) e", u=2, e=2)
             if u < G:
                 nc.vector.tensor_scalar(
-                    out=r16[:], in0=logs[k][:, i], scalar1=shift[:, 0:1], scalar2=None, op0=ALU.subtract
+                    out=r16[:], in0=src, scalar1=shift[:, 0:1], scalar2=None, op0=ALU.subtract
                 )
             else:
                 nc.vector.tensor_scalar(
-                    out=r16[:], in0=logs[k][:, i], scalar1=-1.0, scalar2=shift[:, 0:1], op0=ALU.mult, op1=ALU.add
+                    out=r16[:], in0=src, scalar1=-1.0, scalar2=shift[:, 0:1], op0=ALU.mult, op1=ALU.add
                 )
-            rounded[u] = r16
+            rounded[u] = r16[:].rearrange("p u w e -> p (u w e)").bitcast(F32)
+
+        def round_rows_scalar(u):
+            k, i = group_of[u]
+            r16 = rpool.tile([P, 2, RT * P, 2], BF16, name="r16")
+            src = logs[k][:, i].rearrange("p rt (d u e) -> p u (rt d) e", u=2, e=2)
+            nc.scalar.activation(out=r16[:], in_=src, func=ACT.Identity, scale=-1.0, bias=shift[:, 0:1])
+            rounded[u] = r16[:].rearrange("p u w e -> p (u w e)").bitcast(F32)
 
         def self_term(k, rt):
             units = GROUPS[k]
@@ -125,14 +133,20 @@ def tile_self_l1_kernel(tc, new_source, new_target, out):
                 op0=ALU.subtract, op1=ALU.mult, accum_out=sp[:, mat, rt, k % 5 : k % 5 + 1],
             )
 
-        def transposes(src, kind, u):
+        def transposes(kind, u):
+            mat, g = divmod(u, G)
             pair = []
             for h in range(2):
                 tp = tpool.tile([P, 2, 2 * P], F32, tag="tp" + kind, name="tp")
                 for j in range(2):
-                    words = src[:, 2 * h + j, :].bitcast(F32).rearrange("p (w u) -> p w u", u=2)
+                    rt = 2 * h + j
                     for uu in range(2):
-                        nc.tensor.transpose(tp[:, uu, P * j : P * j + P], words[:, :, uu], ident[:])
+                        if kind == "p":
+                            words = x[mat][:, g, rt, :].bitcast(F32)[:, uu : KP // 2 : 2]
+                        else:
+                            w0 = (uu * RT + rt) * P
+                            words = rounded[u][:, w0 : w0 + P]
+                        nc.tensor.transpose(tp[:, uu, P * j : P * j + P], words, ident[:])
                 pair.append(tp)
             banks[kind, u] = pair
 
@@ -167,17 +181,19 @@ def tile_self_l1_kernel(tc, new_source, new_target, out):
                 )
 
         waiting = []
-        transposes(x[0][:, 0], "p", 0)
+        transposes("p", 0)
         log_rows(0)
         copy_out("p", 0, vector=True)
         for u in range(UNITS):
-            mat, g = divmod(u + 1, G)
-            round_rows(u)
+            if u < UNITS - 1:
+                round_rows(u)
             if u + 1 < UNITS:
-                transposes(x[mat][:, g], "p", u + 1)
-            transposes(rounded[u], "l", u)
+                transposes("p", u + 1)
+            transposes("l", u)
             if u + 1 < UNITS:
                 log_rows(u + 1)
+            if u == UNITS - 2:
+                round_rows_scalar(u + 1)
             if u >= 1:
                 quant(gls[u - 1], "l", lq, u - 1)
             quant(gps[u], "p", pq, u)
@@ -198,10 +214,11 @@ def tile_self_l1_kernel(tc, new_source, new_target, out):
         last = UNITS - 1
         for k, rt, n in waiting:
             self_term(k, rt)
+        for rt in range(RT - 1):
+            self_term(len(GROUPS) - 1, rt)
         quant(gls[last], "l", lq, last)
         passes(last)
-        for rt in range(RT):
-            self_term(len(GROUPS) - 1, rt)
+        self_term(len(GROUPS) - 1, RT - 1)
         nc.vector.tensor_reduce(out=selfs[:], in_=sp[:], axis=AX.X, op=ALU.add)
         nc.vector.tensor_sub(out=ds[:], in0=selfs[:, 0, :], in1=selfs[:, 1, :])
         for col, m in enumerate((0, 2, 3)):

@@ -22,7 +22,12 @@ UNITS = 2 * G
 FLOPS = 2 * 2 * N_ROWS * N_ROWS * D
 
 LN_SCALE = 2.0**62
-GROUPS = ((0,), (1,), (2, 3), (4, 5), (6, 7), (8, 9), (10, 11), (12, 13), (14,), (15,))
+GROUPS = ((0,), (1,), (2, 3), (4, 5), (6, 7), (8, 9), (10, 11), (12, 13), (14, 15))
+FIRST_TARGET_GROUP = 5
+SUMS = 6
+SCALAR_ROUNDS = 14
+SELF_FIRST = 13
+LEAD = 2
 
 
 def tile_self_l1_kernel(tc, new_source, new_target, out):
@@ -31,6 +36,7 @@ def tile_self_l1_kernel(tc, new_source, new_target, out):
         const = ctx.enter_context(tc.tile_pool(name="const", bufs=1))
         xpool = ctx.enter_context(tc.tile_pool(name="xpool", bufs=1))
         npool = ctx.enter_context(tc.tile_pool(name="npool", bufs=4))
+        jpool = ctx.enter_context(tc.tile_pool(name="jpool", bufs=4))
         rpool = ctx.enter_context(tc.tile_pool(name="rpool", bufs=3))
         gpool = ctx.enter_context(tc.tile_pool(name="gpool", bufs=3))
         qpool = ctx.enter_context(tc.tile_pool(name="qpool", bufs=3))
@@ -58,12 +64,13 @@ def tile_self_l1_kernel(tc, new_source, new_target, out):
         make_identity(nc, ident[:])
         mean_w = const.tile([P, P], F32)
         nc.vector.memset(mean_w[:], 1.0 / (N_ROWS * N_ROWS))
-        sp = const.tile([P, 2, RT, 8], F32)
+        sp = const.tile([P, 2, RT, SUMS], F32)
         nc.vector.memset(sp[:], 0.0)
         parts = const.tile([P, 16], F32)
         nc.vector.memset(parts[:], 0.0)
         nc.vector.memset(parts[:, 15:16], 1e-4 / P)
         selfs = const.tile([P, 2, RT], F32)
+        most = const.tile([P, RT], F32)
         ds = const.tile([P, RT], F32)
         junk_a = const.tile([P, N_ROWS], F32)
         xd = const.tile([P, N_ROWS], F32)
@@ -77,10 +84,8 @@ def tile_self_l1_kernel(tc, new_source, new_target, out):
         logs = {}
         rounded = {}
         banks = {}
-        gps = {}
-        gls = {}
-        pq = {}
-        lq = {}
+        grouped = {}
+        quantised = {}
         acc = []
         for m in range(RT):
             acc.append(apool.tile([P, N_ROWS], F32, tag="acc%d" % m, name="acc%d" % m))
@@ -127,10 +132,12 @@ def tile_self_l1_kernel(tc, new_source, new_target, out):
             mat, g0 = divmod(units[0], G)
             n = len(units)
             l32 = logs[k]
+            col = SUMS - 1 if k == len(GROUPS) - 1 else k % FIRST_TARGET_GROUP
+            junk = jpool.tile([P, 2, KP], BF16, name="junk")
             nc.vector.scalar_tensor_tensor(
-                out=l32[:, 0:n, rt, :], in0=l32[:, 0:n, rt, :], scalar=shift[:, 0:1],
+                out=junk[:, 0:n], in0=l32[:, 0:n, rt, :], scalar=shift[:, 0:1],
                 in1=x[mat][:, g0 : g0 + n, rt, :],
-                op0=ALU.subtract, op1=ALU.mult, accum_out=sp[:, mat, rt, k % 5 : k % 5 + 1],
+                op0=ALU.subtract, op1=ALU.mult, accum_out=sp[:, mat, rt, col : col + 1],
             )
 
         def transposes(kind, u):
@@ -151,8 +158,11 @@ def tile_self_l1_kernel(tc, new_source, new_target, out):
             banks[kind, u] = pair
 
         def copy_out(kind, u, vector=False):
-            gp = gpool.tile([P, 4 * N_ROWS], BF16, align_bytes=64, tag="g" + kind, name="gp")
-            gw = gp[:].bitcast(F32).rearrange("p (r u) -> p r u", u=2)
+            if u not in grouped:
+                pair = gpool.tile([P, 2, 4 * N_ROWS], BF16, align_bytes=64, name="pair")
+                grouped[u] = pair
+            half = grouped[u][:, 0 if kind == "p" else 1, :]
+            gw = half.bitcast(F32).rearrange("p (r u) -> p r u", u=2)
             for h in range(2):
                 dst = gw[:, 256 * h : 256 * h + 256, :]
                 src = banks[kind, u][h][:].rearrange("p u r -> p r u")
@@ -160,67 +170,81 @@ def tile_self_l1_kernel(tc, new_source, new_target, out):
                     nc.vector.tensor_copy(out=dst, in_=src)
                 else:
                     nc.scalar.copy(out=dst, in_=src)
-            (gps if kind == "p" else gls)[u] = gp
 
-        def quant(src, kind, store, u):
-            codes = qpool.tile([P, N_ROWS], U32, align_bytes=64, tag="codes" + kind, name="codes")
-            scales = qpool.tile([P, N_ROWS], U8, align_bytes=64, tag="scales" + kind, name="scales")
-            nc.vector.quantize_mx(out=codes[:].bitcast(FP8X4), scales=scales[:], in_=src[:])
-            store[u] = (codes, scales)
+        def quant(u, first=0, n=2):
+            if u not in quantised:
+                codes = qpool.tile([P, 2, N_ROWS], U32, align_bytes=64, name="codes")
+                scales = qpool.tile([P, 2, N_ROWS], U8, align_bytes=64, name="scales")
+                quantised[u] = (codes, scales)
+            codes, scales = quantised[u]
+            halves = slice(first, first + n)
+            nc.vector.quantize_mx(
+                out=codes[:, halves].rearrange("p k r -> p (k r)").bitcast(FP8X4),
+                scales=scales[:, halves].rearrange("p k r -> p (k r)"),
+                in_=grouped[u][:, halves].rearrange("p k c -> p (k c)"),
+            )
 
         def passes(u):
-            pc, ps = pq[u]
-            lc, ls = lq[u]
+            codes, scales = quantised[u]
             for m in range(RT):
                 cols = slice(P * m, P * m + P)
                 nc.tensor.matmul_mx(
                     out=acc[m][:],
-                    lhsT=pc[:, cols].bitcast(FP8X4), lhsT_scale=ps[:, cols],
-                    rhs=lc[:].bitcast(FP8X4), rhs_scale=ls[:],
+                    lhsT=codes[:, 0, cols].bitcast(FP8X4), lhsT_scale=scales[:, 0, cols],
+                    rhs=codes[:, 1, :].bitcast(FP8X4), rhs_scale=scales[:, 1, :],
                     start=(u == 0), stop=(u == UNITS - 1),
                 )
 
         waiting = []
+
+        def self_terms(room):
+            while waiting and room > 0:
+                k, rt = waiting.pop(0)
+                self_term(k, rt)
+                room -= len(GROUPS[k])
+
+        def groups_up_to(u):
+            for k, units in enumerate(GROUPS):
+                if units[-1] == u:
+                    waiting.extend([(k, rt) for rt in range(RT)])
+
+        last = UNITS - 1
         transposes("p", 0)
         log_rows(0)
         copy_out("p", 0, vector=True)
+        for u in range(1, LEAD):
+            log_rows(u)
+        groups_up_to(0)
         for u in range(UNITS):
-            if u < UNITS - 1:
+            if u + LEAD - 1 < UNITS and u + LEAD - 1 > 0:
+                groups_up_to(u + LEAD - 1)
+            if u >= SELF_FIRST:
+                self_terms(RT)
+            if u < SCALAR_ROUNDS:
                 round_rows(u)
-            if u + 1 < UNITS:
+            if u < last:
                 transposes("p", u + 1)
             transposes("l", u)
-            if u + 1 < UNITS:
-                log_rows(u + 1)
-            if u == UNITS - 2:
+            if u + LEAD < UNITS:
+                log_rows(u + LEAD)
+            if SCALAR_ROUNDS <= u + 1 < UNITS:
                 round_rows_scalar(u + 1)
             if u >= 1:
-                quant(gls[u - 1], "l", lq, u - 1)
-            quant(gps[u], "p", pq, u)
-            if u >= 1:
+                quant(u - 1)
                 passes(u - 1)
-            k, i = group_of[u]
-            n = len(GROUPS[k])
-            if i == n - 1 and u < UNITS - 1:
-                waiting += [(k, rt, n) for rt in range(RT)]
-            done = 0
-            while waiting and done < 4:
-                k, rt, n = waiting.pop(0)
-                self_term(k, rt)
-                done += n
-            if u + 1 < UNITS:
+            if u == 0:
+                copy_out("p", 1, vector=True)
+            if u < SELF_FIRST:
+                self_terms(RT)
+            if 0 < u < last:
                 copy_out("p", u + 1)
             copy_out("l", u)
-        last = UNITS - 1
-        for k, rt, n in waiting:
-            self_term(k, rt)
-        for rt in range(RT - 1):
-            self_term(len(GROUPS) - 1, rt)
-        quant(gls[last], "l", lq, last)
+        nc.vector.tensor_reduce(out=selfs[:], in_=sp[:, :, :, 0 : SUMS - 1], axis=AX.X, op=ALU.add)
+        quant(last, 0, 1)
+        nc.vector.tensor_sub(out=most[:], in0=selfs[:, 0, :], in1=selfs[:, 1, :])
+        quant(last, 1, 1)
         passes(last)
-        self_term(len(GROUPS) - 1, RT - 1)
-        nc.vector.tensor_reduce(out=selfs[:], in_=sp[:], axis=AX.X, op=ALU.add)
-        nc.vector.tensor_sub(out=ds[:], in0=selfs[:, 0, :], in1=selfs[:, 1, :])
+        nc.vector.tensor_sub(out=ds[:], in0=most[:], in1=sp[:, 1, :, SUMS - 1])
         for col, m in enumerate((0, 2, 3)):
             nc.scalar.activation(
                 out=junk_a[:], in_=acc[m][:], func=ACT.Abs, scale=-1.0, bias=ds[:, m : m + 1],

@@ -108,8 +108,8 @@ def tile_self_l1_kernel(tc, new_source, new_target, out):
 
         def round_rows(u):
             k, i = group_of[u]
-            r16 = rpool.tile([P, 2, RT * P, 2], BF16, name="r16")
-            src = logs[k][:, i].rearrange("p rt (d u e) -> p u (rt d) e", u=2, e=2)
+            r16 = rpool.tile([P, RT, KP], BF16, name="r16")
+            src = logs[k][:, i]
             if u < G:
                 nc.vector.tensor_scalar(
                     out=r16[:], in0=src, scalar1=shift[:, 0:1], scalar2=None, op0=ALU.subtract
@@ -118,14 +118,14 @@ def tile_self_l1_kernel(tc, new_source, new_target, out):
                 nc.vector.tensor_scalar(
                     out=r16[:], in0=src, scalar1=-1.0, scalar2=shift[:, 0:1], op0=ALU.mult, op1=ALU.add
                 )
-            rounded[u] = r16[:].rearrange("p u w e -> p (u w e)").bitcast(F32)
+            rounded[u] = r16
 
         def round_rows_scalar(u):
             k, i = group_of[u]
-            r16 = rpool.tile([P, 2, RT * P, 2], BF16, name="r16")
-            src = logs[k][:, i].rearrange("p rt (d u e) -> p u (rt d) e", u=2, e=2)
+            r16 = rpool.tile([P, RT, KP], BF16, name="r16")
+            src = logs[k][:, i]
             nc.scalar.activation(out=r16[:], in_=src, func=ACT.Identity, scale=-1.0, bias=shift[:, 0:1])
-            rounded[u] = r16[:].rearrange("p u w e -> p (u w e)").bitcast(F32)
+            rounded[u] = r16
 
         def self_term(k, rt):
             units = GROUPS[k]
@@ -148,11 +148,8 @@ def tile_self_l1_kernel(tc, new_source, new_target, out):
                 for j in range(2):
                     rt = 2 * h + j
                     for uu in range(2):
-                        if kind == "p":
-                            words = x[mat][:, g, rt, :].bitcast(F32)[:, uu : KP // 2 : 2]
-                        else:
-                            w0 = (uu * RT + rt) * P
-                            words = rounded[u][:, w0 : w0 + P]
+                        rows = x[mat][:, g, rt, :] if kind == "p" else rounded[u][:, rt, :]
+                        words = rows.bitcast(F32)[:, uu : KP // 2 : 2]
                         nc.tensor.transpose(tp[:, uu, P * j : P * j + P], words, ident[:])
                 pair.append(tp)
             banks[kind, u] = pair

@@ -51,8 +51,8 @@ def tile_self_l1_kernel(tc, new_source, new_target, out):
             view = dram.rearrange("(rt p) (g w) -> p g rt w", p=P, w=KP)
             for g in range(G):
                 if mat == 0 and g == 0:
-                    nc.sync.dma_start(out=x[0][:, 0, 0:2], in_=view[:, 0, 0:2])
-                    nc.sync.dma_start(out=x[0][:, 0, 2:4], in_=view[:, 0, 2:4])
+                    for rt in range(RT):
+                        nc.sync.dma_start(out=x[0][:, 0, rt], in_=view[:, 0, rt])
                 else:
                     nc.sync.dma_start(out=x[mat][:, g], in_=view[:, g])
 
@@ -98,10 +98,9 @@ def tile_self_l1_kernel(tc, new_source, new_target, out):
                 logs[k] = l32
             l32 = logs[k]
             if u == 0:
-                for h in range(2):
-                    rows = slice(2 * h, 2 * h + 2)
+                for rt in range(RT):
                     nc.scalar.activation(
-                        out=l32[:, i, rows], in_=x[mat][:, g, rows], func=ACT.Ln, scale=LN_SCALE
+                        out=l32[:, i, rt], in_=x[mat][:, g, rt], func=ACT.Ln, scale=LN_SCALE
                     )
             else:
                 nc.scalar.activation(out=l32[:, i], in_=x[mat][:, g], func=ACT.Ln, scale=LN_SCALE)
@@ -144,7 +143,7 @@ def tile_self_l1_kernel(tc, new_source, new_target, out):
             mat, g = divmod(u, G)
             pair = []
             for h in range(2):
-                tp = tpool.tile([P, 2, 2 * P], F32, tag="tp" + kind, name="tp")
+                tp = tpool.tile([P, 2, 2 * P], F32, tag="tpp" if u == UNITS - 1 else "tp" + kind, name="tp")
                 for j in range(2):
                     rt = 2 * h + j
                     for uu in range(2):
@@ -194,8 +193,8 @@ def tile_self_l1_kernel(tc, new_source, new_target, out):
 
         waiting = []
 
-        def self_terms(room):
-            while waiting and room > 0:
+        def self_terms(room, keep=0):
+            while len(waiting) > keep and room > 0:
                 k, rt = waiting.pop(0)
                 self_term(k, rt)
                 room -= len(GROUPS[k])
@@ -215,8 +214,12 @@ def tile_self_l1_kernel(tc, new_source, new_target, out):
         for u in range(UNITS):
             if u + LEAD - 1 < UNITS and u + LEAD - 1 > 0:
                 groups_up_to(u + LEAD - 1)
+            if u == last:
+                nc.vector.tensor_reduce(out=selfs[:], in_=sp[:, :, :, 0 : SUMS - 1], axis=AX.X, op=ALU.add)
             if u >= SELF_FIRST:
-                self_terms(RT)
+                self_terms(RT, 1 if u == last else 0)
+            if u == last:
+                nc.vector.tensor_sub(out=most[:], in0=selfs[:, 0, :], in1=selfs[:, 1, :])
             if u < SCALAR_ROUNDS:
                 round_rows(u)
             if u < last:
@@ -226,7 +229,12 @@ def tile_self_l1_kernel(tc, new_source, new_target, out):
                 log_rows(u + LEAD)
             if SCALAR_ROUNDS <= u + 1 < UNITS:
                 round_rows_scalar(u + 1)
-            if u >= 1:
+            if u == last:
+                quant(last - 1, 0, 1)
+                quant(last, 0, 1)
+                quant(last - 1, 1, 1)
+                passes(last - 1)
+            elif u >= 1:
                 quant(u - 1)
                 passes(u - 1)
             if u == 0:
@@ -236,12 +244,11 @@ def tile_self_l1_kernel(tc, new_source, new_target, out):
             if 0 < u < last:
                 copy_out("p", u + 1)
             copy_out("l", u)
-        nc.vector.tensor_reduce(out=selfs[:], in_=sp[:, :, :, 0 : SUMS - 1], axis=AX.X, op=ALU.add)
-        quant(last, 0, 1)
-        nc.vector.tensor_sub(out=most[:], in0=selfs[:, 0, :], in1=selfs[:, 1, :])
         quant(last, 1, 1)
         passes(last)
-        nc.vector.tensor_sub(out=ds[:], in0=most[:], in1=sp[:, 1, :, SUMS - 1])
+        nc.vector.tensor_sub(out=ds[:, 0:3], in0=most[:, 0:3], in1=sp[:, 1, 0:3, SUMS - 1])
+        self_terms(RT)
+        nc.vector.tensor_sub(out=ds[:, 3:4], in0=most[:, 3:4], in1=sp[:, 1, 3:4, SUMS - 1])
         for col, m in enumerate((0, 2, 3)):
             nc.scalar.activation(
                 out=junk_a[:], in_=acc[m][:], func=ACT.Abs, scale=-1.0, bias=ds[:, m : m + 1],

@@ -22,9 +22,9 @@ UNITS = 2 * G
 FLOPS = 2 * 2 * N_ROWS * N_ROWS * D
 
 LN_SCALE = 2.0**62
-GROUPS = ((0,), (1,), (2, 3), (4, 5), (6, 7), (8, 9), (10, 11), (12, 13), (14, 15))
-FIRST_TARGET_GROUP = 5
-SUMS = 6
+GROUPS = ((0, 1, 2, 3), (4, 5, 6, 7), (8, 9, 10, 11), (12, 13, 14, 15))
+FIRST_TARGET_GROUP = 2
+SUMS = 3
 SCALAR_ROUNDS = 14
 SELF_FIRST = 13
 LEAD = 2
@@ -35,10 +35,10 @@ def tile_self_l1_kernel(tc, new_source, new_target, out):
     with ExitStack() as ctx:
         const = ctx.enter_context(tc.tile_pool(name="const", bufs=1))
         xpool = ctx.enter_context(tc.tile_pool(name="xpool", bufs=1))
-        npool = ctx.enter_context(tc.tile_pool(name="npool", bufs=4))
+        npool = ctx.enter_context(tc.tile_pool(name="npool", bufs=2))
         jpool = ctx.enter_context(tc.tile_pool(name="jpool", bufs=4))
         rpool = ctx.enter_context(tc.tile_pool(name="rpool", bufs=3))
-        gpool = ctx.enter_context(tc.tile_pool(name="gpool", bufs=3))
+        gpool = ctx.enter_context(tc.tile_pool(name="gpool", bufs=4))
         qpool = ctx.enter_context(tc.tile_pool(name="qpool", bufs=3))
         tpool = ctx.enter_context(tc.psum_pool(name="tpool", bufs=2))
         apool = ctx.enter_context(tc.psum_pool(name="apool", bufs=1))
@@ -94,7 +94,7 @@ def tile_self_l1_kernel(tc, new_source, new_target, out):
             mat, g = divmod(u, G)
             k, i = group_of[u]
             if i == 0:
-                l32 = npool.tile([P, 2, RT, KP], F32, name="l32")
+                l32 = npool.tile([P, 4, RT, KP], F32, name="l32")
                 logs[k] = l32
             l32 = logs[k]
             if u == 0:
@@ -132,7 +132,7 @@ def tile_self_l1_kernel(tc, new_source, new_target, out):
             n = len(units)
             l32 = logs[k]
             col = SUMS - 1 if k == len(GROUPS) - 1 else k % FIRST_TARGET_GROUP
-            junk = jpool.tile([P, 2, KP], BF16, name="junk")
+            junk = jpool.tile([P, 4, KP], BF16, name="junk")
             nc.vector.scalar_tensor_tensor(
                 out=junk[:, 0:n], in0=l32[:, 0:n, rt, :], scalar=shift[:, 0:1],
                 in1=x[mat][:, g0 : g0 + n, rt, :],
@@ -192,62 +192,68 @@ def tile_self_l1_kernel(tc, new_source, new_target, out):
                 )
 
         waiting = []
-
-        def self_terms(room, keep=0):
-            while len(waiting) > keep and room > 0:
+        room = [0]
+        def self_terms(keep=0, more=RT):
+            room[0] = min(room[0] + more, 2 * RT)
+            while len(waiting) > keep and room[0] > 0:
                 k, rt = waiting.pop(0)
                 self_term(k, rt)
-                room -= len(GROUPS[k])
-
+                room[0] -= len(GROUPS[k])
         def groups_up_to(u):
             for k, units in enumerate(GROUPS):
                 if units[-1] == u:
                     waiting.extend([(k, rt) for rt in range(RT)])
-
         last = UNITS - 1
         transposes("p", 0)
         log_rows(0)
         copy_out("p", 0, vector=True)
         for u in range(1, LEAD):
             log_rows(u)
-        groups_up_to(0)
+        for u in range(LEAD - 1):
+            groups_up_to(u)
         for u in range(UNITS):
-            if u + LEAD - 1 < UNITS and u + LEAD - 1 > 0:
+            if u + LEAD - 1 < UNITS:
                 groups_up_to(u + LEAD - 1)
             if u == last:
                 nc.vector.tensor_reduce(out=selfs[:], in_=sp[:, :, :, 0 : SUMS - 1], axis=AX.X, op=ALU.add)
-            if u >= SELF_FIRST:
-                self_terms(RT, 1 if u == last else 0)
+            if u >= 16:
+                self_terms(0 if u == last else 0)
             if u == last:
                 nc.vector.tensor_sub(out=most[:], in0=selfs[:, 0, :], in1=selfs[:, 1, :])
-            if u < SCALAR_ROUNDS:
+            if u not in (14, 15):
                 round_rows(u)
             if u < last:
                 transposes("p", u + 1)
             transposes("l", u)
             if u + LEAD < UNITS:
                 log_rows(u + LEAD)
-            if SCALAR_ROUNDS <= u + 1 < UNITS:
+            if u + 1 in (14, 15):
                 round_rows_scalar(u + 1)
             if u == last:
-                quant(last - 1, 0, 1)
+                for w in range(last - 2, last):
+                    quant(w, 0, 1)
                 quant(last, 0, 1)
-                quant(last - 1, 1, 1)
-                passes(last - 1)
-            elif u >= 1:
-                quant(u - 1)
-                passes(u - 1)
-            if u == 0:
-                copy_out("p", 1, vector=True)
-            if u < SELF_FIRST:
-                self_terms(RT)
-            if 0 < u < last:
+                for w in range(last - 2, last):
+                    quant(w, 1, 1)
+                    passes(w)
+            elif u >= 2:
+                quant(u - 2)
+                passes(u - 2)
+            if u + 1 in (0, 1):
+                copy_out("p", u + 1, vector=True)
+            if u in (0,):
+                copy_out("l", u, vector=True)
+            if u < 16:
+                self_terms()
+            if u < last and u + 1 not in (0, 1):
                 copy_out("p", u + 1)
-            copy_out("l", u)
+            if u not in (0,):
+                copy_out("l", u)
         quant(last, 1, 1)
         passes(last)
         nc.vector.tensor_sub(out=ds[:, 0:3], in0=most[:, 0:3], in1=sp[:, 1, 0:3, SUMS - 1])
-        self_terms(RT)
+        self_terms(0, 99)
+        self_terms(0, 99)
         nc.vector.tensor_sub(out=ds[:, 3:4], in0=most[:, 3:4], in1=sp[:, 1, 3:4, SUMS - 1])
         for col, m in enumerate((0, 2, 3)):
             nc.scalar.activation(

from contextlib import ExitStack

import concourse.mybir as mybir
from concourse.masks import make_identity

F32 = mybir.dt.float32
BF16 = mybir.dt.bfloat16
U32 = mybir.dt.uint32
U8 = mybir.dt.uint8
FP8X4 = mybir.dt.float8_e4m3fn_x4
ACT = mybir.ActivationFunctionType
ALU = mybir.AluOpType
AX = mybir.AxisListType

P = 128
N_ROWS = 512
D = 4096
RT = N_ROWS // P
KP = 512
G = D // KP
UNITS = 2 * G
FLOPS = 2 * 2 * N_ROWS * N_ROWS * D

LN_SCALE = 2.0**62
GROUPS = ((0, 1, 2, 3), (4, 5, 6, 7), (8, 9, 10, 11), (12, 13, 14, 15))
FIRST_TARGET_GROUP = 2
SUMS = 3
SCALAR_ROUNDS = 14
SELF_FIRST = 13
LEAD = 2


def tile_self_l1_kernel(tc, new_source, new_target, out):
    nc = tc.nc
    with ExitStack() as ctx:
        const = ctx.enter_context(tc.tile_pool(name="const", bufs=1))
        xpool = ctx.enter_context(tc.tile_pool(name="xpool", bufs=1))
        npool = ctx.enter_context(tc.tile_pool(name="npool", bufs=2))
        jpool = ctx.enter_context(tc.tile_pool(name="jpool", bufs=4))
        rpool = ctx.enter_context(tc.tile_pool(name="rpool", bufs=3))
        gpool = ctx.enter_context(tc.tile_pool(name="gpool", bufs=4))
        qpool = ctx.enter_context(tc.tile_pool(name="qpool", bufs=3))
        tpool = ctx.enter_context(tc.psum_pool(name="tpool", bufs=2))
        apool = ctx.enter_context(tc.psum_pool(name="apool", bufs=1))
        ctx.enter_context(tc.manual_schedule())

        x_src = xpool.tile([P, G, RT, KP], BF16)
        x_tgt = xpool.tile([P, G, RT, KP], BF16)
        x = (x_src, x_tgt)
        for mat, dram in enumerate((new_source, new_target)):
            view = dram.rearrange("(rt p) (g w) -> p g rt w", p=P, w=KP)
            for g in range(G):
                if mat == 0 and g == 0:
                    for rt in range(RT):
                        nc.sync.dma_start(out=x[0][:, 0, rt], in_=view[:, 0, rt])
                else:
                    nc.sync.dma_start(out=x[mat][:, g], in_=view[:, g])

        unit = const.tile([P, 1], F32)
        nc.vector.memset(unit[:], 1.0)
        shift = const.tile([P, 1], F32)
        nc.scalar.activation(out=shift[:], in_=unit[:], func=ACT.Ln, scale=LN_SCALE)
        ident = const.tile([P, P], F32)
        make_identity(nc, ident[:])
        mean_w = const.tile([P, P], F32)
        nc.vector.memset(mean_w[:], 1.0 / (N_ROWS * N_ROWS))
        sp = const.tile([P, 2, RT, SUMS], F32)
        nc.vector.memset(sp[:], 0.0)
        parts = const.tile([P, 16], F32)
        nc.vector.memset(parts[:], 0.0)
        nc.vector.memset(parts[:, 15:16], 1e-4 / P)
        selfs = const.tile([P, 2, RT], F32)
        most = const.tile([P, RT], F32)
        ds = const.tile([P, RT], F32)
        junk_a = const.tile([P, N_ROWS], F32)
        xd = const.tile([P, N_ROWS], F32)
        junk_v = const.tile([P, N_ROWS], F32)
        res = const.tile([P, 1], F32)

        group_of = {}
        for k, units in enumerate(GROUPS):
            for i, u in enumerate(units):
                group_of[u] = (k, i)
        logs = {}
        rounded = {}
        banks = {}
        grouped = {}
        quantised = {}
        acc = []
        for m in range(RT):
            acc.append(apool.tile([P, N_ROWS], F32, tag="acc%d" % m, name="acc%d" % m))

        def log_rows(u):
            mat, g = divmod(u, G)
            k, i = group_of[u]
            if i == 0:
                l32 = npool.tile([P, 4, RT, KP], F32, name="l32")
                logs[k] = l32
            l32 = logs[k]
            if u == 0:
                for rt in range(RT):
                    nc.scalar.activation(
                        out=l32[:, i, rt], in_=x[mat][:, g, rt], func=ACT.Ln, scale=LN_SCALE
                    )
            else:
                nc.scalar.activation(out=l32[:, i], in_=x[mat][:, g], func=ACT.Ln, scale=LN_SCALE)

        def round_rows(u):
            k, i = group_of[u]
            r16 = rpool.tile([P, RT, KP], BF16, name="r16")
            src = logs[k][:, i]
            if u < G:
                nc.vector.tensor_scalar(
                    out=r16[:], in0=src, scalar1=shift[:, 0:1], scalar2=None, op0=ALU.subtract
                )
            else:
                nc.vector.tensor_scalar(
                    out=r16[:], in0=src, scalar1=-1.0, scalar2=shift[:, 0:1], op0=ALU.mult, op1=ALU.add
                )
            rounded[u] = r16

        def round_rows_scalar(u):
            k, i = group_of[u]
            r16 = rpool.tile([P, RT, KP], BF16, name="r16")
            src = logs[k][:, i]
            nc.scalar.activation(out=r16[:], in_=src, func=ACT.Identity, scale=-1.0, bias=shift[:, 0:1])
            rounded[u] = r16

        def self_term(k, rt):
            units = GROUPS[k]
            mat, g0 = divmod(units[0], G)
            n = len(units)
            l32 = logs[k]
            col = SUMS - 1 if k == len(GROUPS) - 1 else k % FIRST_TARGET_GROUP
            junk = jpool.tile([P, 4, KP], BF16, name="junk")
            nc.vector.scalar_tensor_tensor(
                out=junk[:, 0:n], in0=l32[:, 0:n, rt, :], scalar=shift[:, 0:1],
                in1=x[mat][:, g0 : g0 + n, rt, :],
                op0=ALU.subtract, op1=ALU.mult, accum_out=sp[:, mat, rt, col : col + 1],
            )

        def transposes(kind, u):
            mat, g = divmod(u, G)
            pair = []
            for h in range(2):
                tp = tpool.tile([P, 2, 2 * P], F32, tag="tpp" if u == UNITS - 1 else "tp" + kind, name="tp")
                for j in range(2):
                    rt = 2 * h + j
                    for uu in range(2):
                        rows = x[mat][:, g, rt, :] if kind == "p" else rounded[u][:, rt, :]
                        words = rows.bitcast(F32)[:, uu : KP // 2 : 2]
                        nc.tensor.transpose(tp[:, uu, P * j : P * j + P], words, ident[:])
                pair.append(tp)
            banks[kind, u] = pair

        def copy_out(kind, u, vector=False):
            if u not in grouped:
                pair = gpool.tile([P, 2, 4 * N_ROWS], BF16, align_bytes=64, name="pair")
                grouped[u] = pair
            half = grouped[u][:, 0 if kind == "p" else 1, :]
            gw = half.bitcast(F32).rearrange("p (r u) -> p r u", u=2)
            for h in range(2):
                dst = gw[:, 256 * h : 256 * h + 256, :]
                src = banks[kind, u][h][:].rearrange("p u r -> p r u")
                if vector:
                    nc.vector.tensor_copy(out=dst, in_=src)
                else:
                    nc.scalar.copy(out=dst, in_=src)

        def quant(u, first=0, n=2):
            if u not in quantised:
                codes = qpool.tile([P, 2, N_ROWS], U32, align_bytes=64, name="codes")
                scales = qpool.tile([P, 2, N_ROWS], U8, align_bytes=64, name="scales")
                quantised[u] = (codes, scales)
            codes, scales = quantised[u]
            halves = slice(first, first + n)
            nc.vector.quantize_mx(
                out=codes[:, halves].rearrange("p k r -> p (k r)").bitcast(FP8X4),
                scales=scales[:, halves].rearrange("p k r -> p (k r)"),
                in_=grouped[u][:, halves].rearrange("p k c -> p (k c)"),
            )

        def passes(u):
            codes, scales = quantised[u]
            for m in range(RT):
                cols = slice(P * m, P * m + P)
                nc.tensor.matmul_mx(
                    out=acc[m][:],
                    lhsT=codes[:, 0, cols].bitcast(FP8X4), lhsT_scale=scales[:, 0, cols],
                    rhs=codes[:, 1, :].bitcast(FP8X4), rhs_scale=scales[:, 1, :],
                    start=(u == 0), stop=(u == UNITS - 1),
                )

        waiting = []
        room = [0]
        def self_terms(keep=0, more=RT):
            room[0] = min(room[0] + more, 2 * RT)
            while len(waiting) > keep and room[0] > 0:
                k, rt = waiting.pop(0)
                self_term(k, rt)
                room[0] -= len(GROUPS[k])
        def groups_up_to(u):
            for k, units in enumerate(GROUPS):
                if units[-1] == u:
                    waiting.extend([(k, rt) for rt in range(RT)])
        last = UNITS - 1
        transposes("p", 0)
        log_rows(0)
        copy_out("p", 0, vector=True)
        for u in range(1, LEAD):
            log_rows(u)
        for u in range(LEAD - 1):
            groups_up_to(u)
        for u in range(UNITS):
            if u + LEAD - 1 < UNITS:
                groups_up_to(u + LEAD - 1)
            if u == last:
                nc.vector.tensor_reduce(out=selfs[:], in_=sp[:, :, :, 0 : SUMS - 1], axis=AX.X, op=ALU.add)
            if u >= 16:
                self_terms(0 if u == last else 0)
            if u == last:
                nc.vector.tensor_sub(out=most[:], in0=selfs[:, 0, :], in1=selfs[:, 1, :])
            if u not in (14, 15):
                round_rows(u)
            if u < last:
                transposes("p", u + 1)
            transposes("l", u)
            if u + LEAD < UNITS:
                log_rows(u + LEAD)
            if u + 1 in (14, 15):
                round_rows_scalar(u + 1)
            if u == last:
                for w in range(last - 2, last):
                    quant(w, 0, 1)
                quant(last, 0, 1)
                for w in range(last - 2, last):
                    quant(w, 1, 1)
                    passes(w)
            elif u >= 2:
                quant(u - 2)
                passes(u - 2)
            if u + 1 in (0, 1):
                copy_out("p", u + 1, vector=True)
            if u in (0,):
                copy_out("l", u, vector=True)
            if u < 16:
                self_terms()
            if u < last and u + 1 not in (0, 1):
                copy_out("p", u + 1)
            if u not in (0,):
                copy_out("l", u)
        quant(last, 1, 1)
        passes(last)
        nc.vector.tensor_sub(out=ds[:, 0:3], in0=most[:, 0:3], in1=sp[:, 1, 0:3, SUMS - 1])
        self_terms(0, 99)
        self_terms(0, 99)
        nc.vector.tensor_sub(out=ds[:, 3:4], in0=most[:, 3:4], in1=sp[:, 1, 3:4, SUMS - 1])
        for col, m in enumerate((0, 2, 3)):
            nc.scalar.activation(
                out=junk_a[:], in_=acc[m][:], func=ACT.Abs, scale=-1.0, bias=ds[:, m : m + 1],
                accum_out=parts[:, col : col + 1],
            )
        nc.vector.tensor_scalar(out=xd[:], in0=acc[1][:], scalar1=ds[:, 1:2], scalar2=None, op0=ALU.subtract)
        nc.vector.scalar_tensor_tensor(
            out=junk_v[:], in0=xd[:], scalar=-1.0, in1=xd[:], op0=ALU.mult, op1=ALU.max,
            accum_out=parts[:, 8:9],
        )
        tot = tpool.tile([P, 2, 2 * P], F32, tag="tpp", name="tot")
        nc.tensor.matmul(out=tot[:, 0, 0:16], lhsT=mean_w[:], rhs=parts[:], start=True, stop=True)
        nc.vector.tensor_reduce(out=res[:], in_=tot[:, 0, 0:16], axis=AX.X, op=ALU.add)
        dst = out
        while dst.ndim < 2:
            dst = dst.unsqueeze(0)
        nc.sync.dma_start(out=dst, in_=res[0:1, 0:1])
